import numpy as np
import ml_dtypes


def mxq(x, axis, fmt="e4m3"):
    dtype, down = {"e4m3": (ml_dtypes.float8_e4m3fn, 7), "e5m2": (ml_dtypes.float8_e5m2, 14)}[fmt]
    v = np.moveaxis(np.asarray(x, np.float32).astype(ml_dtypes.bfloat16).astype(np.float64), axis, -1)
    blocks = v.reshape(v.shape[:-1] + (-1, 32))
    amax = np.abs(blocks).max(-1, keepdims=True)
    byte = np.maximum(np.where(amax > 0, np.frexp(amax)[1] - 1 + 127, 0) - down, 1)
    scale = np.exp2(byte - 127.0)
    codes = (blocks / scale).astype(np.float32).astype(dtype).astype(np.float64)
    return np.moveaxis((codes * scale).reshape(v.shape), -1, axis)


WIDE = False


def mx_kscale(k):
    if not WIDE:
        return np.ones(k)
    levels = np.array([10, -10, 5, -5, 0])
    a = np.random.permutation(np.resize(levels, k // 512 * 4)).reshape(k // 512, 4)
    idx = np.arange(k)
    return np.exp2(a[idx // 512, idx % 128 // 32])


BF16 = ml_dtypes.bfloat16


def bf(x):
    return np.asarray(x, np.float32).astype(BF16)


def f64(x):
    return np.asarray(x).astype(np.float64)


B, T, H, A = 128, 40, 512, 1024


def softmax_t(z):
    e = np.exp(z - z.max(axis=1, keepdims=True))
    return e / e.sum(axis=1, keepdims=True)


def setup_inputs():
    s = mx_kscale(2 * H)
    return {"ht": bf(np.random.standard_normal((B, H)) * s[:H]),
            "ct": bf(np.random.standard_normal((B, H)) * s[H:]),
            "hi": bf(np.random.standard_normal((B, T, H))),
            "W_as": bf(np.random.standard_normal((2 * H, A)) * 0.7 / np.sqrt(2 * H) / s[:, None]),
            "W_ah": bf(np.random.standard_normal((H, A)) * 0.7 / np.sqrt(H)),
            "ba": bf(np.random.standard_normal((1, A)) * 0.3),
            "v": bf(np.random.standard_normal((1, A)) * 0.5),
            "W_a": bf(np.random.standard_normal((A, H)) * 2.0 / np.sqrt(A))}


def reference(ht, ct, hi, W_as, W_ah, ba, v, W_a):
    hi = f64(hi)
    q = np.concatenate((f64(ht), f64(ct)), axis=-1)
    a_s = mxq(q, 1, "e4m3") @ mxq(f64(W_as), 0, "e4m3")
    ah = mxq(hi, 2, "e4m3") @ mxq(f64(W_ah), 0, "e4m3")
    etk = np.tanh(a_s[:, None, :] + ah + f64(ba))
    etk = mxq(etk, 2, "e4m3") @ mxq(f64(W_a), 0, "e4m3")
    atk = softmax_t(etk)
    return np.sum(atk * hi, axis=1)

@@ -1,0 +1,473 @@
+from contextlib import ExitStack
+
+import concourse.mybir as mybir
+from concourse.masks import make_identity
+
+F32 = mybir.dt.float32
+BF16 = mybir.dt.bfloat16
+U32 = mybir.dt.uint32
+U8 = mybir.dt.uint8
+FP8X4 = mybir.dt.float8_e4m3fn_x4
+ACTF = mybir.ActivationFunctionType
+ALU = mybir.AluOpType
+AX = mybir.AxisListType
+
+P = 128
+B, T, H, A = 128, 40, 512, 1024
+FLOPS = 2 * B * (2 * H) * A + 2 * B * T * H * A + 2 * B * T * A * H
+
+WB = 3
+WR = WB * T
+WIN = 128
+GW = 4
+GB = WB * GW
+NG = 11
+CS = 704
+N_HS = 3
+N_GQ = 3
+TREE = (20, 10)
+EV_ACT = ()
+
+
+def tile_haint_attention_t_kernel(tc, ht, ct, hi, W_as, W_ah, ba, v, W_a, out):
+    nc = tc.nc
+    with ExitStack() as ctx:
+        const = ctx.enter_context(tc.tile_pool(name="const", bufs=1))
+        wraw = ctx.enter_context(tc.tile_pool(name="wraw", bufs=4))
+        wgrp = ctx.enter_context(tc.tile_pool(name="wgrp", bufs=3))
+        hitp = ctx.enter_context(tc.tile_pool(name="hitp", bufs=5))
+        hicp = ctx.enter_context(tc.tile_pool(name="hicp", bufs=3))
+        xpool = ctx.enter_context(tc.tile_pool(name="xpool", bufs=4))
+        gcp = ctx.enter_context(tc.tile_pool(name="gcp", bufs=6))
+        epool = ctx.enter_context(tc.tile_pool(name="epool", bufs=3))
+        small = ctx.enter_context(tc.tile_pool(name="small", bufs=8))
+        ps_t = ctx.enter_context(tc.psum_pool(name="ps_t", bufs=2))
+        ps_1 = ctx.enter_context(tc.psum_pool(name="ps_1", bufs=3))
+        ps_z = ctx.enter_context(tc.psum_pool(name="ps_z", bufs=3))
+
+        def nb_of(G, w):
+            return max(0, min(WB, B - (GB * G + WB * w)))
+
+        def segs_of(G):
+            segs = []
+            for w in range(GW):
+                n = nb_of(G, w)
+                if n == 0:
+                    continue
+                if segs and segs[-1][2] == n:
+                    segs[-1] = (segs[-1][0], segs[-1][1] + 1, n)
+                else:
+                    segs.append((w, 1, n))
+            return segs
+
+        ident_f = const.tile([P, P], F32, name="ident_f")
+        make_identity(nc, ident_f[:])
+        ident_b = const.tile([P, P], BF16, name="ident_b")
+        make_identity(nc, ident_b[:])
+
+        hs = [const.tile([P, GW * H], BF16, name="hs%d" % i) for i in range(N_HS)]
+        ba_t = const.tile([P, P], BF16, name="ba_t")
+        gq = [[const.tile([P, GW * WIN * 4], BF16, name="gq%d_%d" % (i, c), align_bytes=64)
+               for c in range(2)] for i in range(N_GQ)]
+        q_sb = const.tile([P, 2 * H], BF16, name="q_sb")
+        qg_t = const.tile([P, 2 * P * 4], BF16, name="qg_t", align_bytes=64)
+        q_codes = const.tile([P, 2 * P], U32, name="q_codes", align_bytes=64)
+        q_scales = const.tile([P, 2 * P], U8, name="q_scales", align_bytes=64)
+        as_codes = const.tile([P, 2 * A], U32, name="as_codes", align_bytes=64)
+        as_scales = const.tile([P, 2 * A], U8, name="as_scales", align_bytes=64)
+        ah_codes = const.tile([P, A], U32, name="ah_codes", align_bytes=64)
+        ah_scales = const.tile([P, A], U8, name="ah_scales", align_bytes=64)
+        a_codes = const.tile([P, 2 * H], U32, name="a_codes", align_bytes=64)
+        a_scales = const.tile([P, 2 * H], U8, name="a_scales", align_bytes=64)
+        c_sb = const.tile([P, 2 * B * 4], F32, name="c_sb")
+        ba_col = const.tile([P, 8], F32, name="ba_col")
+        den = const.tile([P, 4 * B], F32, name="den")
+        num = const.tile([P, 4 * B], F32, name="num")
+        rden = const.tile([P, 4 * B], F32, name="rden")
+        o_t = const.tile([P, 4 * B], F32, name="o_t")
+        out_sb = const.tile([P, H], F32, name="out_sb")
+
+        hi_rows = hi.rearrange("b t h -> (b t) h")
+        hit = {}
+        hic = {}
+        tps = {}
+        ps1s = {}
+        xs = {}
+        gcs = {}
+        pszs = {}
+        negms = {}
+        es = {}
+
+        ctx.enter_context(tc.manual_schedule())
+
+        def ld(G):
+            if G >= NG:
+                return
+            dst = hs[G % N_HS]
+            for w in range(GW):
+                r0 = (GW * G + w) * WR
+                n = min(P, B * T - r0)
+                if n > 0:
+                    nc.sync.dma_start(out=dst[0:n, w * H:(w + 1) * H], in_=hi_rows[r0:r0 + n, :])
+
+        def tr(G, wp):
+            if G >= NG:
+                return
+            src = hs[G % N_HS]
+            tp = ps_t.tile([P, 512], F32, name="tp", tag="tp")
+            for wl in range(2):
+                w = 2 * wp + wl
+                for u in range(2):
+                    nc.tensor.transpose(
+                        tp[:, (2 * wl + u) * P:(2 * wl + u + 1) * P],
+                        src[:, w * H:(w + 1) * H].bitcast(F32)[:, u * P:(u + 1) * P],
+                        ident_f[:])
+            tps[(G, wp)] = tp
+
+        def ev(G, wp):
+            if G >= NG:
+                return
+            if wp == 0:
+                hit[G] = hitp.tile([P, GW * WIN * 4], BF16, name="hit", tag="hit", align_bytes=64)
+            dst = hit[G][:].bitcast(F32)[:, wp * 512:(wp + 1) * 512].rearrange(
+                "p (w c u) -> p w c u", w=2, c=P, u=2)
+            srcv = tps[(G, wp)][:].rearrange("p (w u c) -> p w c u", w=2, u=2, c=P)
+            if wp in EV_ACT:
+                nc.scalar.copy(out=dst, in_=srcv)
+            else:
+                nc.vector.tensor_copy(out=dst, in_=srcv)
+
+        def qh(G):
+            if G >= NG:
+                return
+            codes = hicp.tile([P, GW * WIN], U32, name="hic", tag="hic", align_bytes=64)
+            scales = hicp.tile([P, GW * WIN], U8, name="his", tag="his", align_bytes=64)
+            nc.vector.quantize_mx(out=codes[:].bitcast(FP8X4), scales=scales[:], in_=hit[G][:])
+            hic[G] = (codes, scales)
+
+        def s1(G, c, w):
+            if G >= NG or nb_of(G, w) == 0:
+                return
+            codes, scales = hic[G]
+            ps1 = ps_1.tile([P, 512], F32, name="ps1", tag="ps1")
+            for j in range(4):
+                m = 4 * c + j
+                nc.tensor.matmul_mx(
+                    out=ps1[:, j * P:(j + 1) * P],
+                    lhsT=ah_codes[:, m * P:(m + 1) * P].bitcast(FP8X4),
+                    lhsT_scale=ah_scales[:, m * P:(m + 1) * P],
+                    rhs=codes[:, w * WIN:(w + 1) * WIN].bitcast(FP8X4),
+                    rhs_scale=scales[:, w * WIN:(w + 1) * WIN],
+                    start=True, stop=True)
+            ps1s[(G, c, w)] = ps1
+
+        def add(G, c, w):
+            if G >= NG or nb_of(G, w) == 0:
+                return
+            n = nb_of(G, w)
+            b0 = GB * G + WB * w
+            if w % 2 == 0:
+                xs[(G, c, w // 2)] = xpool.tile([P, 2 * WR * 4], F32, name="x", tag="x")
+            x = xs[(G, c, w // 2)]
+            x0 = (w % 2) * WR * 4
+            nc.vector.tensor_tensor(
+                out=x[:, x0:x0 + n * T * 4].rearrange("p (b t j) -> p b t j", b=n, t=T, j=4),
+                in0=ps1s[(G, c, w)][:].rearrange("p (j r) -> p j r", j=4)[:, :, 0:n * T].rearrange(
+                    "p j (b t) -> p b t j", b=n),
+                in1=c_sb[:, c * 512 + 4 * b0:c * 512 + 4 * (b0 + n)].rearrange(
+                    "p (b j) -> p b j", j=4).unsqueeze(2).to_broadcast([P, n, T, 4]),
+                op=ALU.add)
+
+        def tanh(G, c, wp):
+            if G >= NG:
+                return
+            ws = [w for w in (2 * wp, 2 * wp + 1) if nb_of(G, w) > 0]
+            if not ws:
+                return
+            x = xs[(G, c, wp)]
+            gv = gq[G % N_GQ][c][:].rearrange("p (w y) -> p w y", w=GW)
+            if all(nb_of(G, w) == WB for w in ws):
+                nw = len(ws)
+                nc.scalar.activation(
+                    out=gv[:, ws[0]:ws[0] + nw, 0:WR * 4],
+                    in_=x[:, 0:nw * WR * 4].rearrange("p (w y) -> p w y", w=nw),
+                    func=ACTF.Tanh)
+            else:
+                for w in ws:
+                    n = nb_of(G, w)
+                    x0 = (w % 2) * WR * 4
+                    nc.scalar.activation(out=gv[:, w, 0:n * T * 4],
+                                         in_=x[:, x0:x0 + n * T * 4], func=ACTF.Tanh)
+
+        def qg(G, c):
+            if G >= NG:
+                return
+            gc = gcp.tile([P, GW * WIN], U32, name="gc", tag="gc", align_bytes=64)
+            gs = gcp.tile([P, GW * WIN], U8, name="gs", tag="gs", align_bytes=64)
+            nc.vector.quantize_mx(out=gc[:].bitcast(FP8X4), scales=gs[:],
+                                  in_=gq[G % N_GQ][c][:])
+            gcs[(G, c)] = (gc, gs)
+
+        def s2(G, jj):
+            if G < 0:
+                return
+            psz = ps_z.tile([P, 512], F32, name="psz", tag="psz")
+            for c in range(2):
+                nc.tensor.matmul_mx(
+                    out=psz[:],
+                    lhsT=a_codes[:, c * H + jj * P:c * H + (jj + 1) * P].bitcast(FP8X4),
+                    lhsT_scale=a_scales[:, c * H + jj * P:c * H + (jj + 1) * P],
+                    rhs=gcs[(G, c)][0][:].bitcast(FP8X4), rhs_scale=gcs[(G, c)][1][:],
+                    start=(c == 0), stop=(c == 1))
+            pszs[(G, jj)] = psz
+
+        def mx(G, jj):
+            if G < 0:
+                return
+            zv = pszs[(G, jj)][:].rearrange("p (w c) -> p w c", w=GW)
+            negm = small.tile([P, GB], F32, name="negm", tag="negm")
+            for (w0, nw, n) in segs_of(G):
+                nc.vector.tensor_reduce(
+                    out=negm[:, WB * w0:WB * w0 + nw * n].rearrange("p (w b) -> p w b", w=nw),
+                    in_=zv[:, w0:w0 + nw, 0:n * T].rearrange("p w (b t) -> p w b t", b=n),
+                    axis=AX.X, op=ALU.max, negate=True)
+            negms[(G, jj)] = negm
+
+        def ex(G, jj):
+            if G < 0:
+                return
+            if jj == 0:
+                es[G] = epool.tile([P, 4 * GB * T], F32, name="e", tag="e")
+            e = es[G]
+            psz = pszs[(G, jj)]
+            negm = negms[(G, jj)]
+            nbg = sum(nb_of(G, w) for w in range(GW))
+            for k in range(nbg):
+                w, b3 = divmod(k, WB)
+                col = jj * B + GB * G + k
+                e0 = jj * GB * T + k * T
+                nc.scalar.activation(
+                    out=e[:, e0:e0 + T],
+                    in_=psz[:, w * WIN + b3 * T:w * WIN + (b3 + 1) * T],
+                    func=ACTF.Exp, bias=negm[:, k:k + 1], scale=1.0,
+                    accum_out=den[:, col:col + 1])
+
+        def pmh(G, h):
+            if G < 0 or G >= NG - 1:
+                return
+            e = es[G]
+            e4 = e[:].rearrange("p (j w r) -> p j w r", j=4, w=GW)[:, 2 * h:2 * h + 2, :, :]
+            hv = hit[G][:].rearrange("p (w c t) -> p t w c", w=GW, c=WIN, t=4)
+            nc.gpsimd.tensor_tensor(out=e4, in0=e4, in1=hv[:, 2 * h:2 * h + 2, :, 0:WR],
+                                    op=ALU.mult)
+            eb = e[:].rearrange("p (x t) -> p x t", t=T)[:, 2 * h * GB:(2 * h + 2) * GB, :]
+            for half in TREE:
+                nc.gpsimd.tensor_tensor(out=eb[:, :, 0:half], in0=eb[:, :, 0:half],
+                                        in1=eb[:, :, half:2 * half], op=ALU.add)
+
+        def rd(G):
+            if G < 0 or G >= NG - 1:
+                return
+            nc.vector.tensor_reduce(
+                out=num[:].rearrange("p (j b) -> p j b", j=4)[:, :, GB * G:GB * (G + 1)],
+                in_=es[G][:].rearrange("p (j b t) -> p j b t", j=4, b=GB)[:, :, :, 0:TREE[-1]],
+                axis=AX.X, op=ALU.add)
+
+        def dm(G, jj):
+            e = es[G]
+            hv = hit[G][:].rearrange("p (w c t) -> p w c t", w=GW, c=WIN, t=4)
+            nbg = sum(nb_of(G, w) for w in range(GW))
+            for (w0, nw, n) in segs_of(G):
+                e0 = jj * GB * T + WR * w0
+                evw = e[:, e0:e0 + nw * n * T].rearrange("p (w r) -> p w r", w=nw)
+                nc.vector.tensor_tensor(out=evw, in0=evw, in1=hv[:, w0:w0 + nw, 0:n * T, jj],
+                                        op=ALU.mult)
+            c0 = jj * B + GB * G
+            nc.vector.tensor_reduce(
+                out=num[:, c0:c0 + nbg],
+                in_=e[:, jj * GB * T:jj * GB * T + nbg * T].rearrange("p (b t) -> p b t", t=T),
+                axis=AX.X, op=ALU.add)
+
+        def norm(b_lo, b_hi):
+            dv = den[:].rearrange("p (j b) -> p j b", j=4)[:, :, b_lo:b_hi]
+            rv = rden[:].rearrange("p (j b) -> p j b", j=4)[:, :, b_lo:b_hi]
+            nv = num[:].rearrange("p (j b) -> p j b", j=4)[:, :, b_lo:b_hi]
+            ov = o_t[:].rearrange("p (j b) -> p j b", j=4)[:, :, b_lo:b_hi]
+            nc.vector.reciprocal(out=rv, in_=dv)
+            nc.vector.tensor_tensor(out=ov, in0=nv, in1=rv, op=ALU.mult)
+
+        nc.vector.memset(ba_t[:], 0.0)
+        for pair in gq:
+            for t in pair:
+                nc.vector.memset(
+                    t[:].rearrange("p (w y) -> p w y", w=GW)[:, :, WR * 4:WIN * 4], 0.0)
+
+        ld(0)
+        nc.sync.dma_start(out=q_sb[:, 0:H], in_=ht)
+        nc.sync.dma_start(out=q_sb[:, H:2 * H], in_=ct)
+        nc.sync.dma_start(out=ba_t[0:8, :], in_=ba.rearrange("o (r c) -> (o r) c", r=8))
+        as_raw = []
+        for g in range(2):
+            r = wraw.tile([P, 4 * A], BF16, name="wr", tag="wr")
+            nc.sync.dma_start(
+                out=r[:].rearrange("p (u e a) -> p u e a", u=2, e=2),
+                in_=W_as[H * g:H * (g + 1), :].rearrange("(u p e) a -> p u e a", u=2, p=P, e=2))
+            as_raw.append(r)
+        ah_raw = wraw.tile([P, 4 * A], BF16, name="wr", tag="wr")
+        nc.sync.dma_start(
+            out=ah_raw[:].rearrange("p (u e a) -> p u e a", u=2, e=2),
+            in_=W_ah.rearrange("(u p e) a -> p u e a", u=2, p=P, e=2))
+        ld(1)
+        a_raw = wraw.tile([P, 8 * H], BF16, name="wr", tag="wr")
+        nc.sync.dma_start(out=a_raw[:].rearrange("p (r h) -> p r h", r=8),
+                          in_=W_a.rearrange("(r p) h -> p r h", p=P))
+        ld(2)
+
+        tr(0, 0)
+        tr(0, 1)
+        ev(0, 0)
+        ev(0, 1)
+        tq = ps_t.tile([P, 512], F32, name="tq", tag="tp")
+        for gu in range(4):
+            nc.tensor.transpose(tq[:, gu * P:(gu + 1) * P],
+                                q_sb[:].bitcast(F32)[:, gu * P:(gu + 1) * P], ident_f[:])
+        nc.vector.tensor_copy(
+            out=qg_t[:].bitcast(F32).rearrange("p (g b u) -> p g b u", g=2, b=P, u=2),
+            in_=tq[:].rearrange("p (g u b) -> p g b u", g=2, u=2, b=P))
+        qh(0)
+        psb = ps_t.tile([P, P], BF16, name="psb", tag="tp")
+        nc.tensor.transpose(psb[:], ba_t[:], ident_b[:])
+        nc.vector.quantize_mx(out=q_codes[:].bitcast(FP8X4), scales=q_scales[:], in_=qg_t[:])
+        nc.vector.tensor_copy(out=ba_col[:], in_=psb[:, 0:8])
+
+        def regroup(raw, grp):
+            s = raw[:].rearrange("p (t a) -> p t a", t=4)
+            d = grp[:].rearrange("p (a t) -> p a t", t=4)
+            nc.vector.tensor_copy(
+                out=d[:, 0:CS, :].rearrange("p (c i) t -> p c t i", i=4),
+                in_=s[:, :, 0:CS].rearrange("p t (c i) -> p c t i", i=4))
+            nc.scalar.copy(
+                out=d[:, CS:A, :].rearrange("p (c i) t -> p c t i", i=4),
+                in_=s[:, :, CS:A].rearrange("p t (c i) -> p c t i", i=4))
+
+        for g in range(2):
+            gt = wgrp.tile([P, 4 * A], BF16, name="wg", tag="wg", align_bytes=64)
+            regroup(as_raw[g], gt)
+            nc.vector.quantize_mx(out=as_codes[:, g * A:(g + 1) * A].bitcast(FP8X4),
+                                  scales=as_scales[:, g * A:(g + 1) * A], in_=gt[:])
+        ah_grp = wgrp.tile([P, 4 * A], BF16, name="wg", tag="wg", align_bytes=64)
+        regroup(ah_raw, ah_grp)
+
+        ps0s = []
+        for c in range(2):
+            ps0 = ps_1.tile([P, 512], F32, name="ps0", tag="ps1")
+            for j in range(4):
+                m = 4 * c + j
+                for g in range(2):
+                    nc.tensor.matmul_mx(
+                        out=ps0[:, j * P:(j + 1) * P],
+                        lhsT=as_codes[:, g * A + m * P:g * A + (m + 1) * P].bitcast(FP8X4),
+                        lhsT_scale=as_scales[:, g * A + m * P:g * A + (m + 1) * P],
+                        rhs=q_codes[:, g * P:(g + 1) * P].bitcast(FP8X4),
+                        rhs_scale=q_scales[:, g * P:(g + 1) * P],
+                        start=(g == 0), stop=(g == 1))
+            ps0s.append(ps0)
+        nc.vector.quantize_mx(out=ah_codes[:].bitcast(FP8X4), scales=ah_scales[:], in_=ah_grp[:])
+        for c in range(2):
+            nc.vector.tensor_tensor(
+                out=c_sb[:, c * 512:(c + 1) * 512].rearrange("p (b j) -> p b j", j=4),
+                in0=ps0s[c][:].rearrange("p (j b) -> p b j", j=4),
+                in1=ba_col[:, 4 * c:4 * c + 4].unsqueeze(1).to_broadcast([P, B, 4]),
+                op=ALU.add)
+
+        a_grp = wgrp.tile([P, 4 * A], BF16, name="wg", tag="wg", align_bytes=64)
+
+        def wa_regroup(c, u):
+            o0 = c * 2048 + u * 1024
+            nc.scalar.copy(
+                out=a_grp[:, o0:o0 + 1024].rearrange("p (e q t) -> p e q t", e=2, q=P, t=4),
+                in_=a_raw[:].rearrange("p (r h) -> p r h", r=8)[
+                    :, 4 * c:4 * c + 4, 256 * u:256 * (u + 1)].rearrange(
+                    "p t (q e) -> p e q t", e=2))
+
+        def wa_quant(c):
+            nc.vector.quantize_mx(out=a_codes[:, c * H:(c + 1) * H].bitcast(FP8X4),
+                                  scales=a_scales[:, c * H:(c + 1) * H],
+                                  in_=a_grp[:, c * 2048:(c + 1) * 2048])
+
+        s1(0, 0, 0)
+        s1(0, 0, 1)
+        for G in range(NG + 1):
+            last = G == NG
+            ld(G + N_HS)
+            pmh(G - 2, 1)
+            s2(G - 1, 0)
+            add(G, 0, 0)
+            s1(G, 0, 2)
+            add(G, 0, 1)
+            tanh(G, 0, 0)
+            s2(G - 1, 1)
+            mx(G - 1, 0)
+            ex(G - 1, 0)
+            if G == 0:
+                wa_regroup(0, 0)
+            s1(G, 0, 3)
+            add(G, 0, 2)
+            tr(G + 1, 0)
+            tr(G + 1, 1)
+            add(G, 0, 3)
+            tanh(G, 0, 1)
+            mx(G - 1, 1)
+            ex(G - 1, 1)
+            pmh(G - 1, 0)
+            if G == 0:
+                wa_regroup(0, 1)
+                wa_regroup(1, 0)
+                wa_regroup(1, 1)
+            if last:
+                norm(0, GB * (NG - 2))
+            s2(G - 1, 2)
+            s1(G, 1, 0)
+            ev(G + 1, 0)
+            s1(G, 1, 1)
+            add(G, 1, 0)
+            mx(G - 1, 2)
+            if last:
+                dm(G - 1, 0)
+            ex(G - 1, 2)
+            if G == 0:
+                wa_quant(0)
+            add(G, 1, 1)
+            tanh(G, 1, 0)
+            s2(G - 1, 3)
+            s1(G, 1, 2)
+            qg(G, 0)
+            mx(G - 1, 3)
+            if last:
+                dm(G - 1, 1)
+            if G == 0:
+                wa_quant(1)
+            s1(G, 1, 3)
+            add(G, 1, 2)
+            add(G, 1, 3)
+            tanh(G, 1, 1)
+            ex(G - 1, 3)
+            ev(G + 1, 1)
+            qh(G + 1)
+            if last:
+                dm(G - 1, 2)
+            rd(G - 2)
+            s1(G + 1, 0, 0)
+            s1(G + 1, 0, 1)
+            qg(G, 1)
+            if last:
+                dm(G - 1, 3)
+
+        norm(GB * (NG - 2), B)
+        pso = ps_z.tile([P, 512], F32, name="pso", tag="psz")
+        for jj in range(4):
+            nc.tensor.transpose(pso[:, jj * P:(jj + 1) * P], o_t[:, jj * P:(jj + 1) * P], ident_f[:])
+        nc.vector.tensor_copy(
+            out=out_sb[:].rearrange("b (u q e) -> b u q e", u=2, q=P, e=2),
+            in_=pso[:].rearrange("b (u e q) -> b u q e", u=2, e=2, q=P))
+        nc.sync.dma_start(out=out, in_=out_sb[:])

@@ -26,7 +26,7 @@ CS = 704
 N_HS = 3
 N_GQ = 3
 TREE = (20, 10)
-EV_ACT = ()
+EV_ACT = (1,)
 
 
 def tile_haint_attention_t_kernel(tc, ht, ct, hi, W_as, W_ah, ba, v, W_a, out):
@@ -84,7 +84,6 @@ def tile_haint_attention_t_kernel(tc, ht, ct, hi, W_as, W_ah, ba, v, W_a, out):
         den = const.tile([P, 4 * B], F32, name="den")
         num = const.tile([P, 4 * B], F32, name="num")
         rden = const.tile([P, 4 * B], F32, name="rden")
-        o_t = const.tile([P, 4 * B], F32, name="o_t")
         out_sb = const.tile([P, H], F32, name="out_sb")
 
         hi_rows = hi.rearrange("b t h -> (b t) h")
@@ -127,7 +126,7 @@ def tile_haint_attention_t_kernel(tc, ht, ct, hi, W_as, W_ah, ba, v, W_a, out):
         def ev(G, wp):
             if G >= NG:
                 return
-            if wp == 0:
+            if G not in hit:
                 hit[G] = hitp.tile([P, GW * WIN * 4], BF16, name="hit", tag="hit", align_bytes=64)
             dst = hit[G][:].bitcast(F32)[:, wp * 512:(wp + 1) * 512].rearrange(
                 "p (w c u) -> p w c u", w=2, c=P, u=2)
@@ -200,7 +199,7 @@ def tile_haint_attention_t_kernel(tc, ht, ct, hi, W_as, W_ah, ba, v, W_a, out):
                                          in_=x[:, x0:x0 + n * T * 4], func=ACTF.Tanh)
 
         def qg(G, c):
-            if G >= NG:
+            if G < 0 or G >= NG:
                 return
             gc = gcp.tile([P, GW * WIN], U32, name="gc", tag="gc", align_bytes=64)
             gs = gcp.tile([P, GW * WIN], U8, name="gs", tag="gs", align_bytes=64)
@@ -265,13 +264,33 @@ def tile_haint_attention_t_kernel(tc, ht, ct, hi, W_as, W_ah, ba, v, W_a, out):
                 nc.gpsimd.tensor_tensor(out=eb[:, :, 0:half], in0=eb[:, :, 0:half],
                                         in1=eb[:, :, half:2 * half], op=ALU.add)
 
-        def rd(G):
-            if G < 0 or G >= NG - 1:
-                return
+        def pmq(G, h):
+            e = es[G]
+            ej = e[:].rearrange("p (j y) -> p j y", j=4)[:, 2 * h:2 * h + 2, :]
+            hv = hit[G][:].rearrange("p (w c t) -> p t w c", w=GW, c=WIN, t=4)[:, 2 * h:2 * h + 2, :, :]
+            nbg = sum(nb_of(G, w) for w in range(GW))
+            for (w0, nw, n) in segs_of(G):
+                evw = ej[:, :, WR * w0:WR * w0 + nw * n * T].rearrange("p j (w r) -> p j w r", w=nw)
+                nc.gpsimd.tensor_tensor(out=evw, in0=evw, in1=hv[:, :, w0:w0 + nw, 0:n * T],
+                                        op=ALU.mult)
+            eb = ej.rearrange("p j (b t) -> p j b t", t=T)[:, :, 0:nbg, :]
+            for half in TREE:
+                nc.gpsimd.tensor_tensor(out=eb[:, :, :, 0:half], in0=eb[:, :, :, 0:half],
+                                        in1=eb[:, :, :, half:2 * half], op=ALU.add)
+
+        def rdj(G, j0, j1):
+            nbg = sum(nb_of(G, w) for w in range(GW))
             nc.vector.tensor_reduce(
-                out=num[:].rearrange("p (j b) -> p j b", j=4)[:, :, GB * G:GB * (G + 1)],
-                in_=es[G][:].rearrange("p (j b t) -> p j b t", j=4, b=GB)[:, :, :, 0:TREE[-1]],
+                out=num[:].rearrange("p (j b) -> p j b", j=4)[:, j0:j1, GB * G:GB * G + nbg],
+                in_=es[G][:].rearrange("p (j b t) -> p j b t", j=4, b=GB)[:, j0:j1, 0:nbg, 0:TREE[-1]],
                 axis=AX.X, op=ALU.add)
+
+        def rd(G):
+            if G >= 0:
+                rdj(G, 0, 4)
+
+        def rdh(G, h):
+            rdj(G, 2 * h, 2 * h + 2)
 
         def dm(G, jj):
             e = es[G]
@@ -288,13 +307,19 @@ def tile_haint_attention_t_kernel(tc, ht, ct, hi, W_as, W_ah, ba, v, W_a, out):
                 in_=e[:, jj * GB * T:jj * GB * T + nbg * T].rearrange("p (b t) -> p b t", t=T),
                 axis=AX.X, op=ALU.add)
 
-        def norm(b_lo, b_hi):
-            dv = den[:].rearrange("p (j b) -> p j b", j=4)[:, :, b_lo:b_hi]
-            rv = rden[:].rearrange("p (j b) -> p j b", j=4)[:, :, b_lo:b_hi]
-            nv = num[:].rearrange("p (j b) -> p j b", j=4)[:, :, b_lo:b_hi]
-            ov = o_t[:].rearrange("p (j b) -> p j b", j=4)[:, :, b_lo:b_hi]
-            nc.vector.reciprocal(out=rv, in_=dv)
-            nc.vector.tensor_tensor(out=ov, in0=nv, in1=rv, op=ALU.mult)
+        def back(src_t):
+            ps = ps_t.tile([P, 512], F32, name="psb2", tag="tp")
+            for jj in range(4):
+                nc.tensor.transpose(ps[:, jj * P:(jj + 1) * P], src_t[:, jj * P:(jj + 1) * P],
+                                    ident_f[:])
+            return ps[:].rearrange("b (u e q) -> b u q e", u=2, e=2, q=P)
+
+        def tr_den():
+            tps["den"] = back(den)
+
+        def recip_den():
+            nc.vector.reciprocal(out=rden[:].rearrange("b (u q e) -> b u q e", u=2, q=P, e=2),
+                                 in_=tps["den"])
 
         nc.vector.memset(ba_t[:], 0.0)
         for pair in gq:
@@ -384,90 +409,130 @@ def tile_haint_attention_t_kernel(tc, ht, ct, hi, W_as, W_ah, ba, v, W_a, out):
 
         def wa_regroup(c, u):
             o0 = c * 2048 + u * 1024
-            nc.scalar.copy(
+            nc.gpsimd.tensor_scalar(
                 out=a_grp[:, o0:o0 + 1024].rearrange("p (e q t) -> p e q t", e=2, q=P, t=4),
-                in_=a_raw[:].rearrange("p (r h) -> p r h", r=8)[
+                in0=a_raw[:].rearrange("p (r h) -> p r h", r=8)[
                     :, 4 * c:4 * c + 4, 256 * u:256 * (u + 1)].rearrange(
-                    "p t (q e) -> p e q t", e=2))
+                    "p t (q e) -> p e q t", e=2),
+                scalar1=1.0, scalar2=0.0, op0=ALU.mult, op1=ALU.add)
 
         def wa_quant(c):
             nc.vector.quantize_mx(out=a_codes[:, c * H:(c + 1) * H].bitcast(FP8X4),
                                   scales=a_scales[:, c * H:(c + 1) * H],
                                   in_=a_grp[:, c * 2048:(c + 1) * 2048])
 
+        for c in range(2):
+            for u in range(2):
+                wa_regroup(c, u)
         s1(0, 0, 0)
         s1(0, 0, 1)
-        for G in range(NG + 1):
-            last = G == NG
-            ld(G + N_HS)
-            pmh(G - 2, 1)
-            s2(G - 1, 0)
+        s1(0, 0, 2)
+        tr(1, 0)
+        tr(1, 1)
+        ld(3)
+        for G in range(NG - 1):
+            ld(G + 4)
             add(G, 0, 0)
-            s1(G, 0, 2)
-            add(G, 0, 1)
-            tanh(G, 0, 0)
-            s2(G - 1, 1)
-            mx(G - 1, 0)
-            ex(G - 1, 0)
-            if G == 0:
-                wa_regroup(0, 0)
             s1(G, 0, 3)
+            ev(G + 1, 1)
+            add(G, 0, 1)
+            s1(G, 1, 0)
+            qg(G - 1, 1)
+            tanh(G, 0, 0)
+            s2(G - 1, 0)
             add(G, 0, 2)
-            tr(G + 1, 0)
-            tr(G + 1, 1)
+            s2(G - 1, 1)
+            ev(G + 1, 0)
             add(G, 0, 3)
             tanh(G, 0, 1)
-            mx(G - 1, 1)
-            ex(G - 1, 1)
-            pmh(G - 1, 0)
-            if G == 0:
-                wa_regroup(0, 1)
-                wa_regroup(1, 0)
-                wa_regroup(1, 1)
-            if last:
-                norm(0, GB * (NG - 2))
-            s2(G - 1, 2)
-            s1(G, 1, 0)
-            ev(G + 1, 0)
             s1(G, 1, 1)
             add(G, 1, 0)
-            mx(G - 1, 2)
-            if last:
-                dm(G - 1, 0)
-            ex(G - 1, 2)
-            if G == 0:
-                wa_quant(0)
+            mx(G - 1, 0)
+            ex(G - 1, 0)
+            mx(G - 1, 1)
             add(G, 1, 1)
-            tanh(G, 1, 0)
-            s2(G - 1, 3)
             s1(G, 1, 2)
-            qg(G, 0)
-            mx(G - 1, 3)
-            if last:
-                dm(G - 1, 1)
-            if G == 0:
-                wa_quant(1)
             s1(G, 1, 3)
+            pmh(G - 2, 1)
+            tr(G + 2, 0)
+            qh(G + 1)
+            s2(G - 1, 2)
+            s1(G + 1, 0, 0)
             add(G, 1, 2)
             add(G, 1, 3)
-            tanh(G, 1, 1)
-            ex(G - 1, 3)
-            ev(G + 1, 1)
-            qh(G + 1)
-            if last:
-                dm(G - 1, 2)
-            rd(G - 2)
-            s1(G + 1, 0, 0)
+            ex(G - 1, 1)
+            qg(G, 0)
+            tanh(G, 1, 0)
+            pmh(G - 1, 0)
+            mx(G - 1, 2)
+            if G == 0:
+                wa_quant(0)
+            s2(G - 1, 3)
+            if G == 0:
+                wa_quant(1)
             s1(G + 1, 0, 1)
-            qg(G, 1)
-            if last:
-                dm(G - 1, 3)
+            mx(G - 1, 3)
+            rd(G - 2)
+            tanh(G, 1, 1)
+            s1(G + 1, 0, 2)
+            ex(G - 1, 2)
+            ex(G - 1, 3)
+            tr(G + 2, 1)
+        G = NG - 1
+        add(G, 0, 0)
+        s1(G, 1, 0)
+        add(G, 0, 1)
+        s1(G, 1, 1)
+        qg(G - 1, 1)
+        tanh(G, 0, 0)
+        s2(G - 1, 0)
+        add(G, 0, 2)
+        add(G, 1, 0)
+        s1(G, 1, 2)
+        add(G, 1, 1)
+        tanh(G, 0, 1)
+        s2(G - 1, 1)
+        tanh(G, 1, 0)
+        pmh(G - 2, 1)
+        mx(G - 1, 0)
+        s2(G - 1, 2)
+        mx(G - 1, 1)
+        ex(G - 1, 0)
+        add(G, 1, 2)
+        qg(G, 0)
+        tanh(G, 1, 1)
+        s2(G - 1, 3)
+        ex(G - 1, 1)
+        mx(G - 1, 2)
+        ex(G - 1, 2)
+        qg(G, 1)
+        mx(G - 1, 3)
+        s2(G, 0)
+        s2(G, 1)
+        mx(G, 0)
+        rd(G - 2)
+        mx(G, 1)
+        ex(G - 1, 3)
+        dm(G - 1, 2)
+        s2(G, 2)
+        mx(G, 2)
+        ex(G, 0)
+        pmh(G - 1, 0)
+        ex(G, 1)
+        s2(G, 3)
+        ex(G, 2)
+        mx(G, 3)
+        dm(G - 1, 3)
+        rdh(G - 1, 0)
+        ex(G, 3)
+        pmq(G, 0)
+        dm(G, 2)
+        dm(G, 3)
+        tr_den()
+        rdh(G, 0)
+        recip_den()
 
-        norm(GB * (NG - 2), B)
-        pso = ps_z.tile([P, 512], F32, name="pso", tag="psz")
-        for jj in range(4):
-            nc.tensor.transpose(pso[:, jj * P:(jj + 1) * P], o_t[:, jj * P:(jj + 1) * P], ident_f[:])
-        nc.vector.tensor_copy(
-            out=out_sb[:].rearrange("b (u q e) -> b u q e", u=2, q=P, e=2),
-            in_=pso[:].rearrange("b (u e q) -> b u q e", u=2, e=2, q=P))
+        nc.vector.tensor_tensor(out=out_sb[:].rearrange("b (u q e) -> b u q e", u=2, q=P, e=2),
+                                in0=back(num), in1=rden[:].rearrange("b (u q e) -> b u q e", u=2, q=P, e=2),
+                                op=ALU.mult)
         nc.sync.dma_start(out=out, in_=out_sb[:])

@@ -22,26 +22,30 @@ WIN = 128
 GW = 4
 GB = WB * GW
 NG = 11
-CS = 704
+HW = 512
+CS_OF = {(0, 0): 288, (1, 0): 288, (2, 0): 288, (0, 1): None, (1, 1): 160, (2, 1): None}
 N_HS = 3
 N_GQ = 3
 TREE = (20, 10)
-EV_ACT = (1,)
+NPT = 4
+EV_S = (1, 2)
 
 
 def tile_haint_attention_t_kernel(tc, ht, ct, hi, W_as, W_ah, ba, v, W_a, out):
     nc = tc.nc
     with ExitStack() as ctx:
         const = ctx.enter_context(tc.tile_pool(name="const", bufs=1))
-        wraw = ctx.enter_context(tc.tile_pool(name="wraw", bufs=4))
+        wraw = ctx.enter_context(tc.tile_pool(name="wraw", bufs=6))
         wgrp = ctx.enter_context(tc.tile_pool(name="wgrp", bufs=3))
+        warp = ctx.enter_context(tc.tile_pool(name="warp", bufs=1))
         hitp = ctx.enter_context(tc.tile_pool(name="hitp", bufs=5))
         hicp = ctx.enter_context(tc.tile_pool(name="hicp", bufs=3))
         xpool = ctx.enter_context(tc.tile_pool(name="xpool", bufs=4))
         gcp = ctx.enter_context(tc.tile_pool(name="gcp", bufs=6))
         epool = ctx.enter_context(tc.tile_pool(name="epool", bufs=3))
         small = ctx.enter_context(tc.tile_pool(name="small", bufs=8))
-        ps_t = ctx.enter_context(tc.psum_pool(name="ps_t", bufs=2))
+        ps_t = ctx.enter_context(tc.psum_pool(name="ps_t", bufs=1))
+        ps_n = ctx.enter_context(tc.psum_pool(name="ps_n", bufs=1))
         ps_1 = ctx.enter_context(tc.psum_pool(name="ps_1", bufs=3))
         ps_z = ctx.enter_context(tc.psum_pool(name="ps_z", bufs=3))
 
@@ -80,6 +84,7 @@ def tile_haint_attention_t_kernel(tc, ht, ct, hi, W_as, W_ah, ba, v, W_a, out):
         a_codes = const.tile([P, 2 * H], U32, name="a_codes", align_bytes=64)
         a_scales = const.tile([P, 2 * H], U8, name="a_scales", align_bytes=64)
         c_sb = const.tile([P, 2 * B * 4], F32, name="c_sb")
+        warm = const.tile([P, 1], F32, name="warm")
         ba_col = const.tile([P, 8], F32, name="ba_col")
         den = const.tile([P, 4 * B], F32, name="den")
         num = const.tile([P, 4 * B], F32, name="num")
@@ -96,8 +101,11 @@ def tile_haint_attention_t_kernel(tc, ht, ct, hi, W_as, W_ah, ba, v, W_a, out):
         pszs = {}
         negms = {}
         es = {}
+        eps = {}
 
         ctx.enter_context(tc.manual_schedule())
+
+        nps = ps_n.tile([P, 512], F32, name="nps")
 
         def ld(G):
             if G >= NG:
@@ -113,7 +121,10 @@ def tile_haint_attention_t_kernel(tc, ht, ct, hi, W_as, W_ah, ba, v, W_a, out):
             if G >= NG:
                 return
             src = hs[G % N_HS]
-            tp = ps_t.tile([P, 512], F32, name="tp", tag="tp")
+            if G < 2 and wp == 1:
+                tp = ps_z.tile([P, 512], F32, name="tp1", tag="psz")
+            else:
+                tp = ps_t.tile([P, 512], F32, name="tp", tag="tp")
             for wl in range(2):
                 w = 2 * wp + wl
                 for u in range(2):
@@ -131,7 +142,7 @@ def tile_haint_attention_t_kernel(tc, ht, ct, hi, W_as, W_ah, ba, v, W_a, out):
             dst = hit[G][:].bitcast(F32)[:, wp * 512:(wp + 1) * 512].rearrange(
                 "p (w c u) -> p w c u", w=2, c=P, u=2)
             srcv = tps[(G, wp)][:].rearrange("p (w u c) -> p w c u", w=2, u=2, c=P)
-            if wp in EV_ACT:
+            if (wp == 1 and G % 2 == 1) or G in EV_S:
                 nc.scalar.copy(out=dst, in_=srcv)
             else:
                 nc.vector.tensor_copy(out=dst, in_=srcv)
@@ -210,7 +221,10 @@ def tile_haint_attention_t_kernel(tc, ht, ct, hi, W_as, W_ah, ba, v, W_a, out):
         def s2(G, jj):
             if G < 0:
                 return
-            psz = ps_z.tile([P, 512], F32, name="psz", tag="psz")
+            if G == NG - 1:
+                psz = ps_1.tile([P, 512], F32, name="psl", tag="ps1")
+            else:
+                psz = ps_z.tile([P, 512], F32, name="psz", tag="psz")
             for c in range(2):
                 nc.tensor.matmul_mx(
                     out=psz[:],
@@ -236,7 +250,10 @@ def tile_haint_attention_t_kernel(tc, ht, ct, hi, W_as, W_ah, ba, v, W_a, out):
             if G < 0:
                 return
             if jj == 0:
-                es[G] = epool.tile([P, 4 * GB * T], F32, name="e", tag="e")
+                if G % 2 == 0:
+                    epair = epool.tile([P, 8 * GB * T], F32, name="e", tag="e")
+                    eps[G // 2] = epair
+                es[G] = eps[G // 2][:].rearrange("p (j g y) -> p g j y", j=4, g=2)[:, G % 2, :, :]
             e = es[G]
             psz = pszs[(G, jj)]
             negm = negms[(G, jj)]
@@ -244,9 +261,8 @@ def tile_haint_attention_t_kernel(tc, ht, ct, hi, W_as, W_ah, ba, v, W_a, out):
             for k in range(nbg):
                 w, b3 = divmod(k, WB)
                 col = jj * B + GB * G + k
-                e0 = jj * GB * T + k * T
                 nc.scalar.activation(
-                    out=e[:, e0:e0 + T],
+                    out=e[:, jj, k * T:(k + 1) * T],
                     in_=psz[:, w * WIN + b3 * T:w * WIN + (b3 + 1) * T],
                     func=ACTF.Exp, bias=negm[:, k:k + 1], scale=1.0,
                     accum_out=den[:, col:col + 1])
@@ -255,18 +271,21 @@ def tile_haint_attention_t_kernel(tc, ht, ct, hi, W_as, W_ah, ba, v, W_a, out):
             if G < 0 or G >= NG - 1:
                 return
             e = es[G]
-            e4 = e[:].rearrange("p (j w r) -> p j w r", j=4, w=GW)[:, 2 * h:2 * h + 2, :, :]
+            e4 = e.rearrange("p j (w r) -> p j w r", w=GW)[:, 2 * h:2 * h + 2, :, :]
             hv = hit[G][:].rearrange("p (w c t) -> p t w c", w=GW, c=WIN, t=4)
             nc.gpsimd.tensor_tensor(out=e4, in0=e4, in1=hv[:, 2 * h:2 * h + 2, :, 0:WR],
                                     op=ALU.mult)
-            eb = e[:].rearrange("p (x t) -> p x t", t=T)[:, 2 * h * GB:(2 * h + 2) * GB, :]
-            for half in TREE:
-                nc.gpsimd.tensor_tensor(out=eb[:, :, 0:half], in0=eb[:, :, 0:half],
-                                        in1=eb[:, :, half:2 * half], op=ALU.add)
+
+        def pa(G, half):
+            if G < 0 or G >= NG - 1:
+                return
+            eb = es[G].rearrange("p j (b t) -> p j b t", t=T)
+            nc.gpsimd.tensor_tensor(out=eb[:, :, :, 0:half], in0=eb[:, :, :, 0:half],
+                                    in1=eb[:, :, :, half:2 * half], op=ALU.add)
 
         def pmq(G, h):
             e = es[G]
-            ej = e[:].rearrange("p (j y) -> p j y", j=4)[:, 2 * h:2 * h + 2, :]
+            ej = e[:, 2 * h:2 * h + 2, :]
             hv = hit[G][:].rearrange("p (w c t) -> p t w c", w=GW, c=WIN, t=4)[:, 2 * h:2 * h + 2, :, :]
             nbg = sum(nb_of(G, w) for w in range(GW))
             for (w0, nw, n) in segs_of(G):
@@ -278,37 +297,83 @@ def tile_haint_attention_t_kernel(tc, ht, ct, hi, W_as, W_ah, ba, v, W_a, out):
                 nc.gpsimd.tensor_tensor(out=eb[:, :, :, 0:half], in0=eb[:, :, :, 0:half],
                                         in1=eb[:, :, :, half:2 * half], op=ALU.add)
 
+        def sm(p, i0, i1):
+            if p < 0 or p >= NPT:
+                return
+            ep = eps[p][:].rearrange("p (x t) -> p t x", t=T)
+            for i in range(i0, i1):
+                nc.tensor.matmul(nps[:, 8 * GB * p:8 * GB * (p + 1)], lhsT=ident_f[:], rhs=ep[:, i, :],
+                                 start=(i == 0), stop=(i == TREE[-1] - 1))
+
         def rdj(G, j0, j1):
             nbg = sum(nb_of(G, w) for w in range(GW))
             nc.vector.tensor_reduce(
                 out=num[:].rearrange("p (j b) -> p j b", j=4)[:, j0:j1, GB * G:GB * G + nbg],
-                in_=es[G][:].rearrange("p (j b t) -> p j b t", j=4, b=GB)[:, j0:j1, 0:nbg, 0:TREE[-1]],
+                in_=es[G].rearrange("p j (b t) -> p j b t", b=GB)[:, j0:j1, 0:nbg, 0:TREE[-1]],
                 axis=AX.X, op=ALU.add)
 
-        def rd(G):
-            if G >= 0:
-                rdj(G, 0, 4)
+        def rdk(G, k):
+            nc.vector.tensor_reduce(
+                out=num[:].rearrange("p (j b) -> p j b", j=4)[:, :, GB * G:GB * G + GB],
+                in_=es[G].rearrange("p j (b t) -> p j b t", b=GB)[:, :, :, 0:k],
+                axis=AX.X, op=ALU.add)
+
+        def rp(G, h):
+            nc.vector.tensor_reduce(
+                out=num[:].rearrange("p (j b) -> p j b", j=4)[:, 2 * h:2 * h + 2, GB * G:GB * G + GB],
+                in_=es[G].rearrange("p j (b t) -> p j b t", b=GB)[:, 2 * h:2 * h + 2, :, :],
+                axis=AX.X, op=ALU.add)
 
         def rdh(G, h):
             rdj(G, 2 * h, 2 * h + 2)
+
+        def rc(G):
+            if G < 0:
+                return
+            b0 = GB * G
+            n = sum(nb_of(G, w) for w in range(GW))
+            dv = den[:].rearrange("p (j b) -> p j b", j=4)
+            rv = rden[:].rearrange("p (j b) -> p j b", j=4)
+            nc.vector.reciprocal(out=rv[:, :, b0:b0 + n], in_=dv[:, :, b0:b0 + n])
+
+        def sm1(G, i0, i1):
+            ev1 = es[G].rearrange("p j (b t) -> p t j b", t=T)
+            c0 = 8 * GB * NPT
+            for i in range(i0, i1):
+                nc.tensor.matmul(nps[:, c0:c0 + 4 * GB].rearrange("p (j b) -> p j b", j=4),
+                                 lhsT=ident_f[:], rhs=ev1[:, i, :, :],
+                                 start=(i == 0), stop=(i == TREE[0] - 1))
+
+        def norm_t(c0, q, b0, nb):
+            w = 4 * nb
+            nc.vector.tensor_tensor(
+                out=num[:].rearrange("p (j b) -> p j b", j=4)[:, :, b0:b0 + q * nb].rearrange(
+                    "p j (q b) -> p q j b", q=q),
+                in0=nps[:, c0:c0 + q * w].rearrange("p (q j b) -> p q j b", q=q, j=4),
+                in1=rden[:].rearrange("p (j b) -> p j b", j=4)[:, :, b0:b0 + q * nb].rearrange(
+                    "p j (q b) -> p q j b", q=q),
+                op=ALU.mult)
+
+        def norm_v(b0, b1):
+            jb = [t[:].rearrange("p (j b) -> p j b", j=4)[:, :, b0:b1] for t in (num, rden)]
+            nc.vector.tensor_tensor(out=jb[0], in0=jb[0], in1=jb[1], op=ALU.mult)
 
         def dm(G, jj):
             e = es[G]
             hv = hit[G][:].rearrange("p (w c t) -> p w c t", w=GW, c=WIN, t=4)
             nbg = sum(nb_of(G, w) for w in range(GW))
             for (w0, nw, n) in segs_of(G):
-                e0 = jj * GB * T + WR * w0
-                evw = e[:, e0:e0 + nw * n * T].rearrange("p (w r) -> p w r", w=nw)
+                evw = e[:, jj, WR * w0:WR * w0 + nw * n * T].rearrange("p (w r) -> p w r", w=nw)
                 nc.vector.tensor_tensor(out=evw, in0=evw, in1=hv[:, w0:w0 + nw, 0:n * T, jj],
                                         op=ALU.mult)
             c0 = jj * B + GB * G
             nc.vector.tensor_reduce(
                 out=num[:, c0:c0 + nbg],
-                in_=e[:, jj * GB * T:jj * GB * T + nbg * T].rearrange("p (b t) -> p b t", t=T),
+                in_=e[:, jj, 0:nbg * T].rearrange("p (b t) -> p b t", t=T),
                 axis=AX.X, op=ALU.add)
 
         def back(src_t):
-            ps = ps_t.tile([P, 512], F32, name="psb2", tag="tp")
+            ps = ps_z.tile([P, 512], F32, name="psb2", tag="psz")
             for jj in range(4):
                 nc.tensor.transpose(ps[:, jj * P:(jj + 1) * P], src_t[:, jj * P:(jj + 1) * P],
                                     ident_f[:])
@@ -321,70 +386,69 @@ def tile_haint_attention_t_kernel(tc, ht, ct, hi, W_as, W_ah, ba, v, W_a, out):
             nc.vector.reciprocal(out=rden[:].rearrange("b (u q e) -> b u q e", u=2, q=P, e=2),
                                  in_=tps["den"])
 
-        nc.vector.memset(ba_t[:], 0.0)
+        nc.gpsimd.memset(ba_t[:], 0.0)
         for pair in gq:
             for t in pair:
-                nc.vector.memset(
+                nc.gpsimd.memset(
                     t[:].rearrange("p (w y) -> p w y", w=GW)[:, :, WR * 4:WIN * 4], 0.0)
 
+        nc.vector.memset(warm[:], 0.0)
+        nc.scalar.activation(out=warm[:], in_=warm[:], func=ACTF.Tanh)
+
+        raw = {}
+
+        def ldw(name, src, h):
+            r = wraw.tile([P, 4 * HW], BF16, name="wr", tag="wr")
+            for u in range(2):
+                nc.sync.dma_start(
+                    out=r[:].rearrange("p (u e a) -> p u e a", u=2, e=2)[:, u, :, :],
+                    in_=src[2 * P * u:2 * P * (u + 1), h * HW:(h + 1) * HW].rearrange(
+                        "(p e) a -> p e a", e=2))
+            raw[(name, h)] = r
+
+        ldw(0, W_as[0:H, :], 0)
+        ldw(1, W_as[H:2 * H, :], 0)
         ld(0)
         nc.sync.dma_start(out=q_sb[:, 0:H], in_=ht)
         nc.sync.dma_start(out=q_sb[:, H:2 * H], in_=ct)
         nc.sync.dma_start(out=ba_t[0:8, :], in_=ba.rearrange("o (r c) -> (o r) c", r=8))
-        as_raw = []
-        for g in range(2):
-            r = wraw.tile([P, 4 * A], BF16, name="wr", tag="wr")
-            nc.sync.dma_start(
-                out=r[:].rearrange("p (u e a) -> p u e a", u=2, e=2),
-                in_=W_as[H * g:H * (g + 1), :].rearrange("(u p e) a -> p u e a", u=2, p=P, e=2))
-            as_raw.append(r)
-        ah_raw = wraw.tile([P, 4 * A], BF16, name="wr", tag="wr")
-        nc.sync.dma_start(
-            out=ah_raw[:].rearrange("p (u e a) -> p u e a", u=2, e=2),
-            in_=W_ah.rearrange("(u p e) a -> p u e a", u=2, p=P, e=2))
+        ldw(2, W_ah, 0)
+        ldw(0, W_as[0:H, :], 1)
+        ldw(1, W_as[H:2 * H, :], 1)
+        ldw(2, W_ah, 1)
         ld(1)
-        a_raw = wraw.tile([P, 8 * H], BF16, name="wr", tag="wr")
+        a_raw = warp.tile([P, 8 * H], BF16, name="a_raw")
         nc.sync.dma_start(out=a_raw[:].rearrange("p (r h) -> p r h", r=8),
                           in_=W_a.rearrange("(r p) h -> p r h", p=P))
         ld(2)
 
-        tr(0, 0)
-        tr(0, 1)
-        ev(0, 0)
-        ev(0, 1)
-        tq = ps_t.tile([P, 512], F32, name="tq", tag="tp")
-        for gu in range(4):
-            nc.tensor.transpose(tq[:, gu * P:(gu + 1) * P],
-                                q_sb[:].bitcast(F32)[:, gu * P:(gu + 1) * P], ident_f[:])
-        nc.vector.tensor_copy(
-            out=qg_t[:].bitcast(F32).rearrange("p (g b u) -> p g b u", g=2, b=P, u=2),
-            in_=tq[:].rearrange("p (g u b) -> p g b u", g=2, u=2, b=P))
-        qh(0)
-        psb = ps_t.tile([P, P], BF16, name="psb", tag="tp")
-        nc.tensor.transpose(psb[:], ba_t[:], ident_b[:])
-        nc.vector.quantize_mx(out=q_codes[:].bitcast(FP8X4), scales=q_scales[:], in_=qg_t[:])
-        nc.vector.tensor_copy(out=ba_col[:], in_=psb[:, 0:8])
+        grp = {}
+        wcodes = {0: as_codes[:, 0:A], 1: as_codes[:, A:2 * A], 2: ah_codes[:]}
+        wscales = {0: as_scales[:, 0:A], 1: as_scales[:, A:2 * A], 2: ah_scales[:]}
 
-        def regroup(raw, grp):
-            s = raw[:].rearrange("p (t a) -> p t a", t=4)
-            d = grp[:].rearrange("p (a t) -> p a t", t=4)
-            nc.vector.tensor_copy(
-                out=d[:, 0:CS, :].rearrange("p (c i) t -> p c t i", i=4),
-                in_=s[:, :, 0:CS].rearrange("p t (c i) -> p c t i", i=4))
-            nc.scalar.copy(
-                out=d[:, CS:A, :].rearrange("p (c i) t -> p c t i", i=4),
-                in_=s[:, :, CS:A].rearrange("p t (c i) -> p c t i", i=4))
+        def regroup(name, h):
+            g = wgrp.tile([P, 4 * HW], BF16, name="wg", tag="wg", align_bytes=64)
+            s = raw[(name, h)][:].rearrange("p (t a) -> p t a", t=4)
+            d = g[:].rearrange("p (a t) -> p a t", t=4)
+            cs = CS_OF[(name, h)]
+            if cs is not None:
+                nc.vector.tensor_copy(
+                    out=d[:, 0:cs, :].rearrange("p (c i) t -> p c t i", i=4),
+                    in_=s[:, :, 0:cs].rearrange("p t (c i) -> p c t i", i=4))
+                nc.scalar.copy(
+                    out=d[:, cs:HW, :].rearrange("p (c i) t -> p c t i", i=4),
+                    in_=s[:, :, cs:HW].rearrange("p t (c i) -> p c t i", i=4))
+            else:
+                nc.gpsimd.tensor_scalar(out=d, in0=s.rearrange("p t a -> p a t"),
+                                        scalar1=1.0, scalar2=0.0, op0=ALU.mult, op1=ALU.add)
+            grp[(name, h)] = g
 
-        for g in range(2):
-            gt = wgrp.tile([P, 4 * A], BF16, name="wg", tag="wg", align_bytes=64)
-            regroup(as_raw[g], gt)
-            nc.vector.quantize_mx(out=as_codes[:, g * A:(g + 1) * A].bitcast(FP8X4),
-                                  scales=as_scales[:, g * A:(g + 1) * A], in_=gt[:])
-        ah_grp = wgrp.tile([P, 4 * A], BF16, name="wg", tag="wg", align_bytes=64)
-        regroup(ah_raw, ah_grp)
+        def quantw(name, h):
+            nc.vector.quantize_mx(out=wcodes[name][:, h * HW:(h + 1) * HW].bitcast(FP8X4),
+                                  scales=wscales[name][:, h * HW:(h + 1) * HW],
+                                  in_=grp[(name, h)][:])
 
-        ps0s = []
-        for c in range(2):
+        def bias_mm(c):
             ps0 = ps_1.tile([P, 512], F32, name="ps0", tag="ps1")
             for j in range(4):
                 m = 4 * c + j
@@ -396,16 +460,63 @@ def tile_haint_attention_t_kernel(tc, ht, ct, hi, W_as, W_ah, ba, v, W_a, out):
                         rhs=q_codes[:, g * P:(g + 1) * P].bitcast(FP8X4),
                         rhs_scale=q_scales[:, g * P:(g + 1) * P],
                         start=(g == 0), stop=(g == 1))
-            ps0s.append(ps0)
-        nc.vector.quantize_mx(out=ah_codes[:].bitcast(FP8X4), scales=ah_scales[:], in_=ah_grp[:])
-        for c in range(2):
+            ps0s[c] = ps0
+
+        def bias_add(c):
             nc.vector.tensor_tensor(
                 out=c_sb[:, c * 512:(c + 1) * 512].rearrange("p (b j) -> p b j", j=4),
                 in0=ps0s[c][:].rearrange("p (j b) -> p b j", j=4),
                 in1=ba_col[:, 4 * c:4 * c + 4].unsqueeze(1).to_broadcast([P, B, 4]),
                 op=ALU.add)
 
-        a_grp = wgrp.tile([P, 4 * A], BF16, name="wg", tag="wg", align_bytes=64)
+        ps0s = {}
+        regroup(0, 0)
+        regroup(1, 0)
+        quantw(0, 0)
+        tr(0, 0)
+        ev(0, 0)
+        tr(0, 1)
+        tq = ps_z.tile([P, 512], F32, name="tq", tag="psz")
+        for gu in range(4):
+            nc.tensor.transpose(tq[:, gu * P:(gu + 1) * P],
+                                q_sb[:].bitcast(F32)[:, gu * P:(gu + 1) * P], ident_f[:])
+        quantw(1, 0)
+        ev(0, 1)
+        nc.scalar.copy(
+            out=qg_t[:].bitcast(F32).rearrange("p (g b u) -> p g b u", g=2, b=P, u=2),
+            in_=tq[:].rearrange("p (g u b) -> p g b u", g=2, u=2, b=P))
+        psb = ps_z.tile([P, P], BF16, name="psb", tag="psz")
+        nc.tensor.transpose(psb[:], ba_t[:], ident_b[:])
+        nc.vector.tensor_copy(out=ba_col[:], in_=psb[:, 0:8])
+        regroup(2, 0)
+        qh(0)
+        nc.vector.quantize_mx(out=q_codes[:].bitcast(FP8X4), scales=q_scales[:], in_=qg_t[:])
+        bias_mm(0)
+        quantw(2, 0)
+        bias_add(0)
+        s1(0, 0, 0)
+        s1(0, 0, 1)
+        s1(0, 0, 2)
+        regroup(0, 1)
+        regroup(2, 1)
+        regroup(1, 1)
+        tr(1, 0)
+        ev(1, 0)
+        tr(1, 1)
+        add(0, 0, 0)
+        s1(0, 0, 3)
+        quantw(0, 1)
+        add(0, 0, 1)
+        quantw(1, 1)
+        bias_mm(1)
+        tanh(0, 0, 0)
+        add(0, 0, 2)
+        ev(1, 1)
+        add(0, 0, 3)
+        quantw(2, 1)
+        bias_add(1)
+        tanh(0, 0, 1)
+        a_grp = warp.tile([P, 4 * A], BF16, name="a_grp", align_bytes=64)
 
         def wa_regroup(c, u):
             o0 = c * 2048 + u * 1024
@@ -424,46 +535,50 @@ def tile_haint_attention_t_kernel(tc, ht, ct, hi, W_as, W_ah, ba, v, W_a, out):
         for c in range(2):
             for u in range(2):
                 wa_regroup(c, u)
-        s1(0, 0, 0)
-        s1(0, 0, 1)
-        s1(0, 0, 2)
-        tr(1, 0)
-        tr(1, 1)
-        ld(3)
         for G in range(NG - 1):
-            ld(G + 4)
-            add(G, 0, 0)
-            s1(G, 0, 3)
-            ev(G + 1, 1)
-            add(G, 0, 1)
-            s1(G, 1, 0)
+            sp = (G - 4) // 2
+            si = 5 * (G % 2)
+            ld(G + 3)
             qg(G - 1, 1)
-            tanh(G, 0, 0)
+            if G > 0:
+                s1(G, 0, 3)
+                ev(G + 1, 1)
+                add(G, 0, 0)
             s2(G - 1, 0)
-            add(G, 0, 2)
-            s2(G - 1, 1)
-            ev(G + 1, 0)
-            add(G, 0, 3)
-            tanh(G, 0, 1)
-            s1(G, 1, 1)
-            add(G, 1, 0)
+            if G > 0:
+                add(G, 0, 1)
+                tanh(G, 0, 0)
+            s1(G, 1, 0)
+            sm(sp, si, si + 1)
             mx(G - 1, 0)
             ex(G - 1, 0)
+            s2(G - 1, 1)
+            if G > 0:
+                add(G, 0, 2)
+                add(G, 0, 3)
+                tanh(G, 0, 1)
+            s1(G, 1, 1)
+            sm(sp, si + 1, si + 2)
+            add(G, 1, 0)
             mx(G - 1, 1)
             add(G, 1, 1)
             s1(G, 1, 2)
             s1(G, 1, 3)
+            sm(sp, si + 2, si + 3)
             pmh(G - 2, 1)
+            pa(G - 2, 20)
             tr(G + 2, 0)
             qh(G + 1)
             s2(G - 1, 2)
             s1(G + 1, 0, 0)
             add(G, 1, 2)
             add(G, 1, 3)
+            ev(G + 2, 0)
             ex(G - 1, 1)
             qg(G, 0)
             tanh(G, 1, 0)
             pmh(G - 1, 0)
+            pa(G - 2, 10)
             mx(G - 1, 2)
             if G == 0:
                 wa_quant(0)
@@ -471,68 +586,86 @@ def tile_haint_attention_t_kernel(tc, ht, ct, hi, W_as, W_ah, ba, v, W_a, out):
             if G == 0:
                 wa_quant(1)
             s1(G + 1, 0, 1)
+            sm(sp, si + 3, si + 4)
             mx(G - 1, 3)
-            rd(G - 2)
+            rc(G - 2)
             tanh(G, 1, 1)
             s1(G + 1, 0, 2)
+            sm(sp, si + 4, si + 5)
             ex(G - 1, 2)
             ex(G - 1, 3)
             tr(G + 2, 1)
         G = NG - 1
+        qg(G - 1, 1)
         add(G, 0, 0)
         s1(G, 1, 0)
         add(G, 0, 1)
         s1(G, 1, 1)
-        qg(G - 1, 1)
         tanh(G, 0, 0)
         s2(G - 1, 0)
+        sm(3, 0, 2)
         add(G, 0, 2)
-        add(G, 1, 0)
         s1(G, 1, 2)
-        add(G, 1, 1)
         tanh(G, 0, 1)
         s2(G - 1, 1)
-        tanh(G, 1, 0)
-        pmh(G - 2, 1)
+        add(G, 1, 0)
         mx(G - 1, 0)
-        s2(G - 1, 2)
-        mx(G - 1, 1)
         ex(G - 1, 0)
+        add(G, 1, 1)
         add(G, 1, 2)
-        qg(G, 0)
+        pmh(G - 2, 1)
+        pa(G - 2, 20)
+        tanh(G, 1, 0)
         tanh(G, 1, 1)
-        s2(G - 1, 3)
+        s2(G - 1, 2)
+        sm(3, 2, 5)
+        mx(G - 1, 1)
         ex(G - 1, 1)
+        qg(G, 0)
         mx(G - 1, 2)
+        s2(G - 1, 3)
+        pmh(G - 1, 0)
         ex(G - 1, 2)
         qg(G, 1)
         mx(G - 1, 3)
+        ex(G - 1, 3)
         s2(G, 0)
         s2(G, 1)
-        mx(G, 0)
-        rd(G - 2)
-        mx(G, 1)
-        ex(G - 1, 3)
-        dm(G - 1, 2)
         s2(G, 2)
-        mx(G, 2)
+        sm(3, 5, 10)
+        pmh(G - 1, 1)
+        mx(G, 0)
         ex(G, 0)
-        pmh(G - 1, 0)
+        mx(G, 1)
         ex(G, 1)
-        s2(G, 3)
+        mx(G, 2)
         ex(G, 2)
+        s2(G, 3)
+        sm1(G - 2, 0, 20)
+        rc(G - 2)
+        rp(G - 1, 0)
+        dm(G, 0)
         mx(G, 3)
-        dm(G - 1, 3)
-        rdh(G - 1, 0)
         ex(G, 3)
-        pmq(G, 0)
+        rc(G - 1)
+        dm(G, 1)
+        rp(G - 1, 1)
+        norm_t(0, NPT, 0, 2 * GB)
         dm(G, 2)
         dm(G, 3)
-        tr_den()
-        rdh(G, 0)
-        recip_den()
+        rc(G)
+        norm_t(8 * GB * NPT, 1, 2 * GB * NPT, GB)
+        norm_v(GB * (G - 1), B)
 
-        nc.vector.tensor_tensor(out=out_sb[:].rearrange("b (u q e) -> b u q e", u=2, q=P, e=2),
-                                in0=back(num), in1=rden[:].rearrange("b (u q e) -> b u q e", u=2, q=P, e=2),
-                                op=ALU.mult)
-        nc.sync.dma_start(out=out, in_=out_sb[:])
+        for u in range(2):
+            ps = ps_z.tile([P, 2 * P], F32, name="pso", tag="psz")
+            for e in range(2):
+                jj = 2 * u + e
+                nc.tensor.transpose(ps[:, e * P:(e + 1) * P], num[:, jj * P:(jj + 1) * P], ident_f[:])
+            ov = out_sb[:, 2 * P * u:2 * P * (u + 1)].rearrange("b (q e) -> b q e", e=2)
+            pv = ps[:].rearrange("b (e q) -> b q e", e=2)
+            if u == 0:
+                nc.vector.tensor_copy(out=ov, in_=pv)
+            else:
+                nc.scalar.copy(out=ov, in_=pv)
+            nc.sync.dma_start(out=out[:, 2 * P * u:2 * P * (u + 1)], in_=out_sb[:, 2 * P * u:2 * P * (u + 1)])

@@ -23,12 +23,11 @@ GW = 4
 GB = WB * GW
 NG = 11
 HW = 512
-CS_OF = {(0, 0): 288, (1, 0): 288, (2, 0): 288, (0, 1): None, (1, 1): 160, (2, 1): None}
+CS = (288, 288)
 N_HS = 3
 N_GQ = 3
-TREE = (20, 10)
 NPT = 4
-EV_S = (1, 2)
+EV_S = (0, 1, 2)
 
 
 def tile_haint_attention_t_kernel(tc, ht, ct, hi, W_as, W_ah, ba, v, W_a, out):
@@ -42,7 +41,10 @@ def tile_haint_attention_t_kernel(tc, ht, ct, hi, W_as, W_ah, ba, v, W_a, out):
         hicp = ctx.enter_context(tc.tile_pool(name="hicp", bufs=3))
         xpool = ctx.enter_context(tc.tile_pool(name="xpool", bufs=4))
         gcp = ctx.enter_context(tc.tile_pool(name="gcp", bufs=6))
-        epool = ctx.enter_context(tc.tile_pool(name="epool", bufs=3))
+        epool = ctx.enter_context(tc.tile_pool(name="epool", bufs=2))
+        prp = ctx.enter_context(tc.tile_pool(name="prp", bufs=2))
+        qrp = ctx.enter_context(tc.tile_pool(name="qrp", bufs=2))
+        rrp = ctx.enter_context(tc.tile_pool(name="rrp", bufs=2))
         small = ctx.enter_context(tc.tile_pool(name="small", bufs=8))
         ps_t = ctx.enter_context(tc.psum_pool(name="ps_t", bufs=1))
         ps_n = ctx.enter_context(tc.psum_pool(name="ps_n", bufs=1))
@@ -101,7 +103,9 @@ def tile_haint_attention_t_kernel(tc, ht, ct, hi, W_as, W_ah, ba, v, W_a, out):
         pszs = {}
         negms = {}
         es = {}
-        eps = {}
+        prs = {}
+        qrs = {}
+        rrs = {}
 
         ctx.enter_context(tc.manual_schedule())
 
@@ -142,7 +146,7 @@ def tile_haint_attention_t_kernel(tc, ht, ct, hi, W_as, W_ah, ba, v, W_a, out):
             dst = hit[G][:].bitcast(F32)[:, wp * 512:(wp + 1) * 512].rearrange(
                 "p (w c u) -> p w c u", w=2, c=P, u=2)
             srcv = tps[(G, wp)][:].rearrange("p (w u c) -> p w c u", w=2, u=2, c=P)
-            if (wp == 1 and G % 2 == 1) or G in EV_S:
+            if G in EV_S:
                 nc.scalar.copy(out=dst, in_=srcv)
             else:
                 nc.vector.tensor_copy(out=dst, in_=srcv)
@@ -221,7 +225,7 @@ def tile_haint_attention_t_kernel(tc, ht, ct, hi, W_as, W_ah, ba, v, W_a, out):
         def s2(G, jj):
             if G < 0:
                 return
-            if G == NG - 1:
+            if G == NG - 1 and jj < 3:
                 psz = ps_1.tile([P, 512], F32, name="psl", tag="ps1")
             else:
                 psz = ps_z.tile([P, 512], F32, name="psz", tag="psz")
@@ -239,21 +243,18 @@ def tile_haint_attention_t_kernel(tc, ht, ct, hi, W_as, W_ah, ba, v, W_a, out):
                 return
             zv = pszs[(G, jj)][:].rearrange("p (w c) -> p w c", w=GW)
             negm = small.tile([P, GB], F32, name="negm", tag="negm")
-            for (w0, nw, n) in segs_of(G):
-                nc.vector.tensor_reduce(
-                    out=negm[:, WB * w0:WB * w0 + nw * n].rearrange("p (w b) -> p w b", w=nw),
-                    in_=zv[:, w0:w0 + nw, 0:n * T].rearrange("p w (b t) -> p w b t", b=n),
-                    axis=AX.X, op=ALU.max, negate=True)
+            nw = sum(1 for w in range(GW) if nb_of(G, w) > 0)
+            nc.vector.tensor_reduce(
+                out=negm[:, 0:WB * nw].rearrange("p (w b) -> p w b", w=nw),
+                in_=zv[:, 0:nw, 0:WR].rearrange("p w (b t) -> p w b t", b=WB),
+                axis=AX.X, op=ALU.max, negate=True)
             negms[(G, jj)] = negm
 
         def ex(G, jj):
             if G < 0:
                 return
             if jj == 0:
-                if G % 2 == 0:
-                    epair = epool.tile([P, 8 * GB * T], F32, name="e", tag="e")
-                    eps[G // 2] = epair
-                es[G] = eps[G // 2][:].rearrange("p (j g y) -> p g j y", j=4, g=2)[:, G % 2, :, :]
+                es[G] = epool.tile([P, 4 * GB * T], F32, name="e", tag="e")
             e = es[G]
             psz = pszs[(G, jj)]
             negm = negms[(G, jj)]
@@ -262,70 +263,76 @@ def tile_haint_attention_t_kernel(tc, ht, ct, hi, W_as, W_ah, ba, v, W_a, out):
                 w, b3 = divmod(k, WB)
                 col = jj * B + GB * G + k
                 nc.scalar.activation(
-                    out=e[:, jj, k * T:(k + 1) * T],
+                    out=e[:, (jj * GB + k) * T:(jj * GB + k + 1) * T],
                     in_=psz[:, w * WIN + b3 * T:w * WIN + (b3 + 1) * T],
                     func=ACTF.Exp, bias=negm[:, k:k + 1], scale=1.0,
                     accum_out=den[:, col:col + 1])
 
-        def pmh(G, h):
-            if G < 0 or G >= NG - 1:
+        def tok(dst, src):
+            nc.vector.tensor_copy(out=dst, in_=src)
+
+        def tok_g(c, G):
+            w = GW - 1
+            while nb_of(G, w) == 0:
+                w -= 1
+            return gq[G % N_GQ][c][:].rearrange("p (w y) -> p w y", w=GW)[:, w, 0:1]
+
+        def mul_tok(G, src):
+            if G < 0:
                 return
-            e = es[G]
-            e4 = e.rearrange("p j (w r) -> p j w r", w=GW)[:, 2 * h:2 * h + 2, :, :]
+            prs[G] = prp.tile([P, 4 * GB * T], F32, name="pr", tag="pr")
+            tok(prs[G][:, 0:1], src)
+
+        def mul(G, h0=0, h1=4):
+            if G < 0:
+                return
             hv = hit[G][:].rearrange("p (w c t) -> p t w c", w=GW, c=WIN, t=4)
-            nc.gpsimd.tensor_tensor(out=e4, in0=e4, in1=hv[:, 2 * h:2 * h + 2, :, 0:WR],
-                                    op=ALU.mult)
+            nc.gpsimd.tensor_tensor(
+                out=prs[G][:].rearrange("p (j w r) -> p j w r", j=4, w=GW)[:, h0:h1, :, :],
+                in0=es[G][:].rearrange("p (j w r) -> p j w r", j=4, w=GW)[:, h0:h1, :, :],
+                in1=hv[:, h0:h1, :, 0:WR], op=ALU.mult)
 
-        def pa(G, half):
-            if G < 0 or G >= NG - 1:
+        def a20_tok(G, src):
+            if G < 0:
                 return
-            eb = es[G].rearrange("p j (b t) -> p j b t", t=T)
-            nc.gpsimd.tensor_tensor(out=eb[:, :, :, 0:half], in0=eb[:, :, :, 0:half],
-                                    in1=eb[:, :, :, half:2 * half], op=ALU.add)
+            qrs[G] = qrp.tile([P, 4 * GB * 20], F32, name="qr", tag="qr")
+            tok(qrs[G][:, 0:1], src)
 
-        def pmq(G, h):
-            e = es[G]
-            ej = e[:, 2 * h:2 * h + 2, :]
-            hv = hit[G][:].rearrange("p (w c t) -> p t w c", w=GW, c=WIN, t=4)[:, 2 * h:2 * h + 2, :, :]
-            nbg = sum(nb_of(G, w) for w in range(GW))
-            for (w0, nw, n) in segs_of(G):
-                evw = ej[:, :, WR * w0:WR * w0 + nw * n * T].rearrange("p j (w r) -> p j w r", w=nw)
-                nc.gpsimd.tensor_tensor(out=evw, in0=evw, in1=hv[:, :, w0:w0 + nw, 0:n * T],
-                                        op=ALU.mult)
-            eb = ej.rearrange("p j (b t) -> p j b t", t=T)[:, :, 0:nbg, :]
-            for half in TREE:
-                nc.gpsimd.tensor_tensor(out=eb[:, :, :, 0:half], in0=eb[:, :, :, 0:half],
-                                        in1=eb[:, :, :, half:2 * half], op=ALU.add)
+        def a20(G):
+            if G < 0:
+                return
+            pv = prs[G][:].rearrange("p (x t) -> p x t", t=T)
+            nc.gpsimd.tensor_tensor(out=qrs[G][:].rearrange("p (x t) -> p x t", t=20),
+                                    in0=pv[:, :, 0:20], in1=pv[:, :, 20:40], op=ALU.add)
+
+        def a10_tok(G, src):
+            if G < 0:
+                return
+            if G % 2 == 0:
+                rrs[G // 2] = rrp.tile([P, 8 * GB * 10], F32, name="rr", tag="rr")
+            g0 = (G % 2) * GB * 10
+            tok(rrs[G // 2][:, g0:g0 + 1], src)
+
+        def a10(G):
+            if G < 0:
+                return
+            qv = qrs[G][:].rearrange("p (j b t) -> p j b t", j=4, t=20)
+            rv = rrs[G // 2][:].rearrange("p (j g b t) -> p j g b t", j=4, g=2, t=10)[:, :, G % 2, :, :]
+            nc.gpsimd.tensor_tensor(out=rv, in0=qv[:, :, :, 0:10], in1=qv[:, :, :, 10:20], op=ALU.add)
 
         def sm(p, i0, i1):
             if p < 0 or p >= NPT:
                 return
-            ep = eps[p][:].rearrange("p (x t) -> p t x", t=T)
+            rp_ = rrs[p][:].rearrange("p (x t) -> p t x", t=10)
             for i in range(i0, i1):
-                nc.tensor.matmul(nps[:, 8 * GB * p:8 * GB * (p + 1)], lhsT=ident_f[:], rhs=ep[:, i, :],
-                                 start=(i == 0), stop=(i == TREE[-1] - 1))
+                nc.tensor.matmul(nps[:, 8 * GB * p:8 * GB * (p + 1)], lhsT=ident_f[:], rhs=rp_[:, i, :],
+                                 start=(i == 0), stop=(i == 9))
 
-        def rdj(G, j0, j1):
-            nbg = sum(nb_of(G, w) for w in range(GW))
-            nc.vector.tensor_reduce(
-                out=num[:].rearrange("p (j b) -> p j b", j=4)[:, j0:j1, GB * G:GB * G + nbg],
-                in_=es[G].rearrange("p j (b t) -> p j b t", b=GB)[:, j0:j1, 0:nbg, 0:TREE[-1]],
-                axis=AX.X, op=ALU.add)
-
-        def rdk(G, k):
-            nc.vector.tensor_reduce(
-                out=num[:].rearrange("p (j b) -> p j b", j=4)[:, :, GB * G:GB * G + GB],
-                in_=es[G].rearrange("p j (b t) -> p j b t", b=GB)[:, :, :, 0:k],
-                axis=AX.X, op=ALU.add)
-
-        def rp(G, h):
-            nc.vector.tensor_reduce(
-                out=num[:].rearrange("p (j b) -> p j b", j=4)[:, 2 * h:2 * h + 2, GB * G:GB * G + GB],
-                in_=es[G].rearrange("p j (b t) -> p j b t", b=GB)[:, 2 * h:2 * h + 2, :, :],
-                axis=AX.X, op=ALU.add)
-
-        def rdh(G, h):
-            rdj(G, 2 * h, 2 * h + 2)
+        def sm1(G, i0, i1):
+            q1 = qrs[G][:].rearrange("p (x t) -> p t x", t=20)
+            for i in range(i0, i1):
+                nc.tensor.matmul(nps[:, 4 * GB * G:4 * GB * (G + 1)], lhsT=ident_f[:], rhs=q1[:, i, :],
+                                 start=(i == 0), stop=(i == 19))
 
         def rc(G):
             if G < 0:
@@ -335,14 +342,6 @@ def tile_haint_attention_t_kernel(tc, ht, ct, hi, W_as, W_ah, ba, v, W_a, out):
             dv = den[:].rearrange("p (j b) -> p j b", j=4)
             rv = rden[:].rearrange("p (j b) -> p j b", j=4)
             nc.vector.reciprocal(out=rv[:, :, b0:b0 + n], in_=dv[:, :, b0:b0 + n])
-
-        def sm1(G, i0, i1):
-            ev1 = es[G].rearrange("p j (b t) -> p t j b", t=T)
-            c0 = 8 * GB * NPT
-            for i in range(i0, i1):
-                nc.tensor.matmul(nps[:, c0:c0 + 4 * GB].rearrange("p (j b) -> p j b", j=4),
-                                 lhsT=ident_f[:], rhs=ev1[:, i, :, :],
-                                 start=(i == 0), stop=(i == TREE[0] - 1))
 
         def norm_t(c0, q, b0, nb):
             w = 4 * nb
@@ -358,33 +357,34 @@ def tile_haint_attention_t_kernel(tc, ht, ct, hi, W_as, W_ah, ba, v, W_a, out):
             jb = [t[:].rearrange("p (j b) -> p j b", j=4)[:, :, b0:b1] for t in (num, rden)]
             nc.vector.tensor_tensor(out=jb[0], in0=jb[0], in1=jb[1], op=ALU.mult)
 
-        def dm(G, jj):
-            e = es[G]
+        def rp(G, h):
+            nc.vector.tensor_reduce(
+                out=num[:].rearrange("p (j b) -> p j b", j=4)[:, 2 * h:2 * h + 2, GB * G:GB * G + GB],
+                in_=prs[G][:].rearrange("p (j b t) -> p j b t", j=4, b=GB)[:, 2 * h:2 * h + 2, :, :],
+                axis=AX.X, op=ALU.add)
+
+        def dmm(G, jj, eng):
             hv = hit[G][:].rearrange("p (w c t) -> p w c t", w=GW, c=WIN, t=4)
-            nbg = sum(nb_of(G, w) for w in range(GW))
             for (w0, nw, n) in segs_of(G):
-                evw = e[:, jj, WR * w0:WR * w0 + nw * n * T].rearrange("p (w r) -> p w r", w=nw)
-                nc.vector.tensor_tensor(out=evw, in0=evw, in1=hv[:, w0:w0 + nw, 0:n * T, jj],
-                                        op=ALU.mult)
+                e0 = jj * GB * T + WR * w0
+                evw = es[G][:, e0:e0 + nw * n * T].rearrange("p (w r) -> p w r", w=nw)
+                eng.tensor_tensor(out=evw, in0=evw, in1=hv[:, w0:w0 + nw, 0:n * T, jj], op=ALU.mult)
+
+        def dmsS(G, jj):
+            nbg = sum(nb_of(G, w) for w in range(GW))
+            for k in range(nbg):
+                e0 = (jj * GB + k) * T
+                c0 = jj * B + GB * G + k
+                nc.scalar.activation(out=es[G][:, e0:e0 + T], in_=es[G][:, e0:e0 + T], func=ACTF.Copy,
+                                     accum_out=num[:, c0:c0 + 1])
+
+        def dms(G, jj):
+            nbg = sum(nb_of(G, w) for w in range(GW))
             c0 = jj * B + GB * G
             nc.vector.tensor_reduce(
                 out=num[:, c0:c0 + nbg],
-                in_=e[:, jj, 0:nbg * T].rearrange("p (b t) -> p b t", t=T),
+                in_=es[G][:, jj * GB * T:jj * GB * T + nbg * T].rearrange("p (b t) -> p b t", t=T),
                 axis=AX.X, op=ALU.add)
-
-        def back(src_t):
-            ps = ps_z.tile([P, 512], F32, name="psb2", tag="psz")
-            for jj in range(4):
-                nc.tensor.transpose(ps[:, jj * P:(jj + 1) * P], src_t[:, jj * P:(jj + 1) * P],
-                                    ident_f[:])
-            return ps[:].rearrange("b (u e q) -> b u q e", u=2, e=2, q=P)
-
-        def tr_den():
-            tps["den"] = back(den)
-
-        def recip_den():
-            nc.vector.reciprocal(out=rden[:].rearrange("b (u q e) -> b u q e", u=2, q=P, e=2),
-                                 in_=tps["den"])
 
         nc.gpsimd.memset(ba_t[:], 0.0)
         for pair in gq:
@@ -430,17 +430,13 @@ def tile_haint_attention_t_kernel(tc, ht, ct, hi, W_as, W_ah, ba, v, W_a, out):
             g = wgrp.tile([P, 4 * HW], BF16, name="wg", tag="wg", align_bytes=64)
             s = raw[(name, h)][:].rearrange("p (t a) -> p t a", t=4)
             d = g[:].rearrange("p (a t) -> p a t", t=4)
-            cs = CS_OF[(name, h)]
-            if cs is not None:
-                nc.vector.tensor_copy(
-                    out=d[:, 0:cs, :].rearrange("p (c i) t -> p c t i", i=4),
-                    in_=s[:, :, 0:cs].rearrange("p t (c i) -> p c t i", i=4))
-                nc.scalar.copy(
-                    out=d[:, cs:HW, :].rearrange("p (c i) t -> p c t i", i=4),
-                    in_=s[:, :, cs:HW].rearrange("p t (c i) -> p c t i", i=4))
-            else:
-                nc.gpsimd.tensor_scalar(out=d, in0=s.rearrange("p t a -> p a t"),
-                                        scalar1=1.0, scalar2=0.0, op0=ALU.mult, op1=ALU.add)
+            cs = CS[h]
+            nc.vector.tensor_copy(
+                out=d[:, 0:cs, :].rearrange("p (c i) t -> p c t i", i=4),
+                in_=s[:, :, 0:cs].rearrange("p t (c i) -> p c t i", i=4))
+            nc.scalar.copy(
+                out=d[:, cs:HW, :].rearrange("p (c i) t -> p c t i", i=4),
+                in_=s[:, :, cs:HW].rearrange("p t (c i) -> p c t i", i=4))
             grp[(name, h)] = g
 
         def quantw(name, h):
@@ -468,6 +464,21 @@ def tile_haint_attention_t_kernel(tc, ht, ct, hi, W_as, W_ah, ba, v, W_a, out):
                 in0=ps0s[c][:].rearrange("p (j b) -> p b j", j=4),
                 in1=ba_col[:, 4 * c:4 * c + 4].unsqueeze(1).to_broadcast([P, B, 4]),
                 op=ALU.add)
+
+        a_grp = warp.tile([P, 4 * A], BF16, name="a_grp", align_bytes=64)
+
+        def wa_regroup(c, u):
+            o0 = c * 2048 + u * 1024
+            nc.scalar.copy(
+                out=a_grp[:, o0:o0 + 1024].rearrange("p (e q t) -> p e q t", e=2, q=P, t=4),
+                in_=a_raw[:].rearrange("p (r h) -> p r h", r=8)[
+                    :, 4 * c:4 * c + 4, 256 * u:256 * (u + 1)].rearrange(
+                    "p t (q e) -> p e q t", e=2))
+
+        def wa_quant(c):
+            nc.vector.quantize_mx(out=a_codes[:, c * H:(c + 1) * H].bitcast(FP8X4),
+                                  scales=a_scales[:, c * H:(c + 1) * H],
+                                  in_=a_grp[:, c * 2048:(c + 1) * 2048])
 
         ps0s = {}
         regroup(0, 0)
@@ -516,146 +527,146 @@ def tile_haint_attention_t_kernel(tc, ht, ct, hi, W_as, W_ah, ba, v, W_a, out):
         quantw(2, 1)
         bias_add(1)
         tanh(0, 0, 1)
-        a_grp = warp.tile([P, 4 * A], BF16, name="a_grp", align_bytes=64)
-
-        def wa_regroup(c, u):
-            o0 = c * 2048 + u * 1024
-            nc.gpsimd.tensor_scalar(
-                out=a_grp[:, o0:o0 + 1024].rearrange("p (e q t) -> p e q t", e=2, q=P, t=4),
-                in0=a_raw[:].rearrange("p (r h) -> p r h", r=8)[
-                    :, 4 * c:4 * c + 4, 256 * u:256 * (u + 1)].rearrange(
-                    "p t (q e) -> p e q t", e=2),
-                scalar1=1.0, scalar2=0.0, op0=ALU.mult, op1=ALU.add)
-
-        def wa_quant(c):
-            nc.vector.quantize_mx(out=a_codes[:, c * H:(c + 1) * H].bitcast(FP8X4),
-                                  scales=a_scales[:, c * H:(c + 1) * H],
-                                  in_=a_grp[:, c * 2048:(c + 1) * 2048])
-
-        for c in range(2):
-            for u in range(2):
-                wa_regroup(c, u)
+        wa_regroup(0, 0)
         for G in range(NG - 1):
             sp = (G - 4) // 2
             si = 5 * (G % 2)
             ld(G + 3)
-            qg(G - 1, 1)
             if G > 0:
-                s1(G, 0, 3)
-                ev(G + 1, 1)
+                a10_tok(G - 3, tok_g(1, G - 1))
+                qg(G - 1, 1)
+                a10(G - 3)
                 add(G, 0, 0)
-            s2(G - 1, 0)
-            if G > 0:
-                add(G, 0, 1)
+                if G == 1:
+                    wa_quant(0)
+                    add(G, 0, 1)
+                    wa_quant(1)
+                s2(G - 1, 0)
+                s1(G, 0, 3)
+                rc(G - 3)
+                s2(G - 1, 1)
+                if G > 1:
+                    add(G, 0, 1)
                 tanh(G, 0, 0)
             s1(G, 1, 0)
-            sm(sp, si, si + 1)
-            mx(G - 1, 0)
-            ex(G - 1, 0)
-            s2(G - 1, 1)
+            mul_tok(G - 2, hit[G + 1][:, 2 * WIN * 4:2 * WIN * 4 + 1])
+            qh(G + 1)
+            mul(G - 2)
+            s2(G - 1, 2)
             if G > 0:
                 add(G, 0, 2)
                 add(G, 0, 3)
                 tanh(G, 0, 1)
             s1(G, 1, 1)
-            sm(sp, si + 1, si + 2)
-            add(G, 1, 0)
-            mx(G - 1, 1)
-            add(G, 1, 1)
+            sm(sp, si, si + 1)
+            mx(G - 1, 0)
+            ex(G - 1, 0)
             s1(G, 1, 2)
+            add(G, 1, 0)
             s1(G, 1, 3)
-            sm(sp, si + 2, si + 3)
-            pmh(G - 2, 1)
-            pa(G - 2, 20)
             tr(G + 2, 0)
-            qh(G + 1)
-            s2(G - 1, 2)
-            s1(G + 1, 0, 0)
-            add(G, 1, 2)
-            add(G, 1, 3)
-            ev(G + 2, 0)
-            ex(G - 1, 1)
-            qg(G, 0)
+            sm(sp, si + 1, si + 2)
+            add(G, 1, 1)
             tanh(G, 1, 0)
-            pmh(G - 1, 0)
-            pa(G - 2, 10)
-            mx(G - 1, 2)
-            if G == 0:
-                wa_quant(0)
+            mx(G - 1, 1)
+            s1(G + 1, 0, 0)
+            sm(sp, si + 2, si + 3)
+            add(G, 1, 2)
             s2(G - 1, 3)
-            if G == 0:
-                wa_quant(1)
             s1(G + 1, 0, 1)
-            sm(sp, si + 3, si + 4)
-            mx(G - 1, 3)
-            rc(G - 2)
+            add(G, 1, 3)
             tanh(G, 1, 1)
+            if G == 0:
+                wa_regroup(0, 1)
+                wa_regroup(1, 0)
+            ex(G - 1, 1)
+            a20_tok(G - 2, tok_g(0, G))
+            qg(G, 0)
+            a20(G - 2)
+            ev(G + 2, 0)
             s1(G + 1, 0, 2)
-            sm(sp, si + 4, si + 5)
-            ex(G - 1, 2)
-            ex(G - 1, 3)
             tr(G + 2, 1)
+            sm(sp, si + 3, si + 5)
+            mx(G - 1, 2)
+            ex(G - 1, 2)
+            mx(G - 1, 3)
+            ex(G - 1, 3)
+            if G == 0:
+                wa_regroup(1, 1)
+            ev(G + 2, 1)
         G = NG - 1
-        qg(G - 1, 1)
         add(G, 0, 0)
         s1(G, 1, 0)
+        a10_tok(G - 3, tok_g(1, G - 1))
+        qg(G - 1, 1)
+        a10(G - 3)
+        s2(G - 1, 0)
         add(G, 0, 1)
         s1(G, 1, 1)
+        s2(G - 1, 1)
         tanh(G, 0, 0)
-        s2(G - 1, 0)
-        sm(3, 0, 2)
         add(G, 0, 2)
         s1(G, 1, 2)
         tanh(G, 0, 1)
-        s2(G - 1, 1)
-        add(G, 1, 0)
+        s2(G - 1, 2)
+        sm(3, 0, 3)
+        mul_tok(G - 2, gq[(G - 1) % N_GQ][1][:, 0:1])
+        mul(G - 2, 0, 2)
         mx(G - 1, 0)
         ex(G - 1, 0)
+        add(G, 1, 0)
         add(G, 1, 1)
         add(G, 1, 2)
-        pmh(G - 2, 1)
-        pa(G - 2, 20)
+        tok(prs[G - 2][:, 2 * GB * T:2 * GB * T + 1], tok_g(0, G))
+        qg(G, 0)
+        mul(G - 2, 2, 4)
         tanh(G, 1, 0)
         tanh(G, 1, 1)
-        s2(G - 1, 2)
-        sm(3, 2, 5)
         mx(G - 1, 1)
-        ex(G - 1, 1)
-        qg(G, 0)
-        mx(G - 1, 2)
+        sm(3, 3, 4)
         s2(G - 1, 3)
-        pmh(G - 1, 0)
+        ex(G - 1, 1)
+        mx(G - 1, 2)
         ex(G - 1, 2)
-        qg(G, 1)
+        sm(3, 4, 7)
         mx(G - 1, 3)
         ex(G - 1, 3)
+        rc(G - 3)
+        prs[G - 1] = prp.tile([P, 4 * GB * T], F32, name="pr", tag="pr")
+        tok(prs[G - 1][:, 0:1], tok_g(1, G))
+        qg(G, 1)
+        mul(G - 1, 0, 2)
         s2(G, 0)
         s2(G, 1)
         s2(G, 2)
-        sm(3, 5, 10)
-        pmh(G - 1, 1)
+        s2(G, 3)
+        sm(3, 7, 10)
+        rc(G - 2)
         mx(G, 0)
         ex(G, 0)
         mx(G, 1)
         ex(G, 1)
         mx(G, 2)
         ex(G, 2)
-        s2(G, 3)
-        sm1(G - 2, 0, 20)
-        rc(G - 2)
-        rp(G - 1, 0)
-        dm(G, 0)
+        mul(G - 1, 2, 4)
+        rp(G - 2, 0)
         mx(G, 3)
         ex(G, 3)
+        rp(G - 2, 1)
+        rp(G - 1, 0)
+        dmm(G, 0, nc.gpsimd)
+        dmsS(G, 0)
+        dmm(G, 1, nc.gpsimd)
+        dmsS(G, 1)
         rc(G - 1)
-        dm(G, 1)
         rp(G - 1, 1)
         norm_t(0, NPT, 0, 2 * GB)
-        dm(G, 2)
-        dm(G, 3)
+        dmm(G, 2, nc.vector)
+        dmm(G, 3, nc.vector)
+        dms(G, 2)
         rc(G)
-        norm_t(8 * GB * NPT, 1, 2 * GB * NPT, GB)
-        norm_v(GB * (G - 1), B)
+        dms(G, 3)
+        norm_v(2 * GB * NPT, B)
 
         for u in range(2):
             ps = ps_z.tile([P, 2 * P], F32, name="pso", tag="psz")

@@ -23,11 +23,11 @@ GW = 4
 GB = WB * GW
 NG = 11
 HW = 512
-CS = (288, 288)
+CS = (256, 224)
 N_HS = 3
 N_GQ = 3
 NPT = 4
-EV_S = (0, 1, 2)
+EV_S = (0, 1)
 
 
 def tile_haint_attention_t_kernel(tc, ht, ct, hi, W_as, W_ah, ba, v, W_a, out):
@@ -469,11 +469,14 @@ def tile_haint_attention_t_kernel(tc, ht, ct, hi, W_as, W_ah, ba, v, W_a, out):
 
         def wa_regroup(c, u):
             o0 = c * 2048 + u * 1024
-            nc.scalar.copy(
-                out=a_grp[:, o0:o0 + 1024].rearrange("p (e q t) -> p e q t", e=2, q=P, t=4),
-                in_=a_raw[:].rearrange("p (r h) -> p r h", r=8)[
-                    :, 4 * c:4 * c + 4, 256 * u:256 * (u + 1)].rearrange(
-                    "p t (q e) -> p e q t", e=2))
+            dst = a_grp[:, o0:o0 + 1024].rearrange("p (e q t) -> p e q t", e=2, q=P, t=4)
+            wsrc = a_raw[:].rearrange("p (r h) -> p r h", r=8)[
+                :, 4 * c:4 * c + 4, 256 * u:256 * (u + 1)].rearrange("p t (q e) -> p e q t", e=2)
+            if (c, u) == (0, 1):
+                nc.gpsimd.tensor_scalar(out=dst, in0=wsrc, scalar1=1.0, scalar2=0.0,
+                                        op0=ALU.mult, op1=ALU.add)
+            else:
+                nc.scalar.copy(out=dst, in_=wsrc)
 
         def wa_quant(c):
             nc.vector.quantize_mx(out=a_codes[:, c * H:(c + 1) * H].bitcast(FP8X4),
@@ -537,21 +540,31 @@ def tile_haint_attention_t_kernel(tc, ht, ct, hi, W_as, W_ah, ba, v, W_a, out):
                 qg(G - 1, 1)
                 a10(G - 3)
                 add(G, 0, 0)
-                if G == 1:
-                    wa_quant(0)
-                    add(G, 0, 1)
-                    wa_quant(1)
+            if G == 1:
+                wa_quant(0)
+                add(G, 0, 1)
+                s1(G, 0, 3)
+                tanh(G, 0, 0)
+                wa_quant(1)
+            if G > 0:
                 s2(G - 1, 0)
+            if G > 1:
                 s1(G, 0, 3)
                 rc(G - 3)
+            if G > 0:
                 s2(G - 1, 1)
-                if G > 1:
-                    add(G, 0, 1)
+            if G > 1:
+                add(G, 0, 1)
                 tanh(G, 0, 0)
             s1(G, 1, 0)
-            mul_tok(G - 2, hit[G + 1][:, 2 * WIN * 4:2 * WIN * 4 + 1])
-            qh(G + 1)
-            mul(G - 2)
+            if G == 0:
+                tok(a_grp[:, 1024:1025], hit[1][:, 2 * WIN * 4:2 * WIN * 4 + 1])
+            if G != 1:
+                mul_tok(G - 2, hit[G + 1][:, 2 * WIN * 4:2 * WIN * 4 + 1])
+                qh(G + 1)
+                mul(G - 2)
+            if G == 0:
+                wa_regroup(0, 1)
             s2(G - 1, 2)
             if G > 0:
                 add(G, 0, 2)
@@ -561,6 +574,9 @@ def tile_haint_attention_t_kernel(tc, ht, ct, hi, W_as, W_ah, ba, v, W_a, out):
             sm(sp, si, si + 1)
             mx(G - 1, 0)
             ex(G - 1, 0)
+            if G == 1:
+                ev(G + 1, 1)
+                qh(G + 1)
             s1(G, 1, 2)
             add(G, 1, 0)
             s1(G, 1, 3)
@@ -577,8 +593,8 @@ def tile_haint_attention_t_kernel(tc, ht, ct, hi, W_as, W_ah, ba, v, W_a, out):
             add(G, 1, 3)
             tanh(G, 1, 1)
             if G == 0:
-                wa_regroup(0, 1)
                 wa_regroup(1, 0)
+                wa_regroup(1, 1)
             ex(G - 1, 1)
             a20_tok(G - 2, tok_g(0, G))
             qg(G, 0)
@@ -591,9 +607,8 @@ def tile_haint_attention_t_kernel(tc, ht, ct, hi, W_as, W_ah, ba, v, W_a, out):
             ex(G - 1, 2)
             mx(G - 1, 3)
             ex(G - 1, 3)
-            if G == 0:
-                wa_regroup(1, 1)
-            ev(G + 2, 1)
+            if G > 0:
+                ev(G + 2, 1)
         G = NG - 1
         add(G, 0, 0)
         s1(G, 1, 0)

@@ -26,6 +26,7 @@ HW = 512
 CS = (256, 224)
 N_HS = 3
 N_GQ = 3
+N_HIT = 5
 NPT = 4
 EV_S = (0, 1)
 
@@ -37,7 +38,6 @@ def tile_haint_attention_t_kernel(tc, ht, ct, hi, W_as, W_ah, ba, v, W_a, out):
         wraw = ctx.enter_context(tc.tile_pool(name="wraw", bufs=6))
         wgrp = ctx.enter_context(tc.tile_pool(name="wgrp", bufs=3))
         warp = ctx.enter_context(tc.tile_pool(name="warp", bufs=1))
-        hitp = ctx.enter_context(tc.tile_pool(name="hitp", bufs=5))
         hicp = ctx.enter_context(tc.tile_pool(name="hicp", bufs=3))
         xpool = ctx.enter_context(tc.tile_pool(name="xpool", bufs=4))
         gcp = ctx.enter_context(tc.tile_pool(name="gcp", bufs=6))
@@ -75,6 +75,8 @@ def tile_haint_attention_t_kernel(tc, ht, ct, hi, W_as, W_ah, ba, v, W_a, out):
         ba_t = const.tile([P, P], BF16, name="ba_t")
         gq = [[const.tile([P, GW * WIN * 4], BF16, name="gq%d_%d" % (i, c), align_bytes=64)
                for c in range(2)] for i in range(N_GQ)]
+        hits = [const.tile([P, GW * WIN * 4], BF16, name="hit%d" % i, align_bytes=64)
+                for i in range(N_HIT)]
         q_sb = const.tile([P, 2 * H], BF16, name="q_sb")
         qg_t = const.tile([P, 2 * P * 4], BF16, name="qg_t", align_bytes=64)
         q_codes = const.tile([P, 2 * P], U32, name="q_codes", align_bytes=64)
@@ -141,11 +143,10 @@ def tile_haint_attention_t_kernel(tc, ht, ct, hi, W_as, W_ah, ba, v, W_a, out):
         def ev(G, wp):
             if G >= NG:
                 return
-            if G not in hit:
-                hit[G] = hitp.tile([P, GW * WIN * 4], BF16, name="hit", tag="hit", align_bytes=64)
+            hit[G] = hits[G % N_HIT]
             dst = hit[G][:].bitcast(F32)[:, wp * 512:(wp + 1) * 512].rearrange(
-                "p (w c u) -> p w c u", w=2, c=P, u=2)
-            srcv = tps[(G, wp)][:].rearrange("p (w u c) -> p w c u", w=2, u=2, c=P)
+                "p (w c u) -> p w c u", w=2, c=P, u=2)[:, :, 0:WR, :]
+            srcv = tps[(G, wp)][:].rearrange("p (w u c) -> p w c u", w=2, u=2, c=P)[:, :, 0:WR, :]
             if G in EV_S:
                 nc.scalar.copy(out=dst, in_=srcv)
             else:
@@ -286,6 +287,8 @@ def tile_haint_attention_t_kernel(tc, ht, ct, hi, W_as, W_ah, ba, v, W_a, out):
         def mul(G, h0=0, h1=4):
             if G < 0:
                 return
+            if G not in prs:
+                prs[G] = prp.tile([P, 4 * GB * T], F32, name="pr", tag="pr")
             hv = hit[G][:].rearrange("p (w c t) -> p t w c", w=GW, c=WIN, t=4)
             nc.gpsimd.tensor_tensor(
                 out=prs[G][:].rearrange("p (j w r) -> p j w r", j=4, w=GW)[:, h0:h1, :, :],
@@ -329,10 +332,10 @@ def tile_haint_attention_t_kernel(tc, ht, ct, hi, W_as, W_ah, ba, v, W_a, out):
                                  start=(i == 0), stop=(i == 9))
 
         def sm1(G, i0, i1):
-            q1 = qrs[G][:].rearrange("p (x t) -> p t x", t=20)
+            q1 = prs[G][:].rearrange("p (x t) -> p t x", t=T)
             for i in range(i0, i1):
-                nc.tensor.matmul(nps[:, 4 * GB * G:4 * GB * (G + 1)], lhsT=ident_f[:], rhs=q1[:, i, :],
-                                 start=(i == 0), stop=(i == 19))
+                nc.tensor.matmul(nps[:, 4 * GB * G:4 * GB * G + 2 * GB], lhsT=ident_f[:],
+                                 rhs=q1[:, i, 0:2 * GB], start=(i == 0), stop=(i == T - 1))
 
         def rc(G):
             if G < 0:
@@ -357,10 +360,10 @@ def tile_haint_attention_t_kernel(tc, ht, ct, hi, W_as, W_ah, ba, v, W_a, out):
             jb = [t[:].rearrange("p (j b) -> p j b", j=4)[:, :, b0:b1] for t in (num, rden)]
             nc.vector.tensor_tensor(out=jb[0], in0=jb[0], in1=jb[1], op=ALU.mult)
 
-        def rp(G, h):
+        def rp(G, j0, j1):
             nc.vector.tensor_reduce(
-                out=num[:].rearrange("p (j b) -> p j b", j=4)[:, 2 * h:2 * h + 2, GB * G:GB * G + GB],
-                in_=prs[G][:].rearrange("p (j b t) -> p j b t", j=4, b=GB)[:, 2 * h:2 * h + 2, :, :],
+                out=num[:].rearrange("p (j b) -> p j b", j=4)[:, j0:j1, GB * G:GB * G + GB],
+                in_=prs[G][:].rearrange("p (j b t) -> p j b t", j=4, b=GB)[:, j0:j1, :, :],
                 axis=AX.X, op=ALU.add)
 
         def dmm(G, jj, eng):
@@ -370,13 +373,12 @@ def tile_haint_attention_t_kernel(tc, ht, ct, hi, W_as, W_ah, ba, v, W_a, out):
                 evw = es[G][:, e0:e0 + nw * n * T].rearrange("p (w r) -> p w r", w=nw)
                 eng.tensor_tensor(out=evw, in0=evw, in1=hv[:, w0:w0 + nw, 0:n * T, jj], op=ALU.mult)
 
-        def dmsS(G, jj):
+        def dmsS(G, jj, src):
             nbg = sum(nb_of(G, w) for w in range(GW))
             for k in range(nbg):
-                e0 = (jj * GB + k) * T
+                v = src[:, (jj * GB + k) * T:(jj * GB + k + 1) * T]
                 c0 = jj * B + GB * G + k
-                nc.scalar.activation(out=es[G][:, e0:e0 + T], in_=es[G][:, e0:e0 + T], func=ACTF.Copy,
-                                     accum_out=num[:, c0:c0 + 1])
+                nc.scalar.activation(out=v, in_=v, func=ACTF.Copy, accum_out=num[:, c0:c0 + 1])
 
         def dms(G, jj):
             nbg = sum(nb_of(G, w) for w in range(GW))
@@ -387,10 +389,9 @@ def tile_haint_attention_t_kernel(tc, ht, ct, hi, W_as, W_ah, ba, v, W_a, out):
                 axis=AX.X, op=ALU.add)
 
         nc.gpsimd.memset(ba_t[:], 0.0)
-        for pair in gq:
-            for t in pair:
-                nc.gpsimd.memset(
-                    t[:].rearrange("p (w y) -> p w y", w=GW)[:, :, WR * 4:WIN * 4], 0.0)
+        for t in hits + [t for pair in gq for t in pair]:
+            nc.gpsimd.memset(
+                t[:].rearrange("p (w y) -> p w y", w=GW)[:, :, WR * 4:WIN * 4], 0.0)
 
         nc.vector.memset(warm[:], 0.0)
         nc.scalar.activation(out=warm[:], in_=warm[:], func=ACTF.Tanh)
@@ -550,7 +551,6 @@ def tile_haint_attention_t_kernel(tc, ht, ct, hi, W_as, W_ah, ba, v, W_a, out):
                 s2(G - 1, 0)
             if G > 1:
                 s1(G, 0, 3)
-                rc(G - 3)
             if G > 0:
                 s2(G - 1, 1)
             if G > 1:
@@ -560,7 +560,6 @@ def tile_haint_attention_t_kernel(tc, ht, ct, hi, W_as, W_ah, ba, v, W_a, out):
             if G == 0:
                 tok(a_grp[:, 1024:1025], hit[1][:, 2 * WIN * 4:2 * WIN * 4 + 1])
             if G != 1:
-                mul_tok(G - 2, hit[G + 1][:, 2 * WIN * 4:2 * WIN * 4 + 1])
                 qh(G + 1)
                 mul(G - 2)
             if G == 0:
@@ -646,7 +645,6 @@ def tile_haint_attention_t_kernel(tc, ht, ct, hi, W_as, W_ah, ba, v, W_a, out):
         sm(3, 4, 7)
         mx(G - 1, 3)
         ex(G - 1, 3)
-        rc(G - 3)
         prs[G - 1] = prp.tile([P, 4 * GB * T], F32, name="pr", tag="pr")
         tok(prs[G - 1][:, 0:1], tok_g(1, G))
         qg(G, 1)
@@ -656,7 +654,6 @@ def tile_haint_attention_t_kernel(tc, ht, ct, hi, W_as, W_ah, ba, v, W_a, out):
         s2(G, 2)
         s2(G, 3)
         sm(3, 7, 10)
-        rc(G - 2)
         mx(G, 0)
         ex(G, 0)
         mx(G, 1)
@@ -664,23 +661,23 @@ def tile_haint_attention_t_kernel(tc, ht, ct, hi, W_as, W_ah, ba, v, W_a, out):
         mx(G, 2)
         ex(G, 2)
         mul(G - 1, 2, 4)
-        rp(G - 2, 0)
+        rp(G - 2, 0, 2)
         mx(G, 3)
         ex(G, 3)
-        rp(G - 2, 1)
-        rp(G - 1, 0)
+        rp(G - 2, 2, 4)
+        rp(G - 1, 0, 2)
+        nc.scalar.activation(out=rden[:], in_=den[:], func=ACTF.Abs_reciprocal_sqrt)
+        nc.scalar.activation(out=rden[:], in_=rden[:], func=ACTF.Square)
         dmm(G, 0, nc.gpsimd)
-        dmsS(G, 0)
-        dmm(G, 1, nc.gpsimd)
-        dmsS(G, 1)
-        rc(G - 1)
-        rp(G - 1, 1)
-        norm_t(0, NPT, 0, 2 * GB)
+        rp(G - 1, 2, 4)
+        dmm(G, 1, nc.vector)
         dmm(G, 2, nc.vector)
         dmm(G, 3, nc.vector)
+        dms(G, 0)
+        dms(G, 1)
         dms(G, 2)
-        rc(G)
         dms(G, 3)
+        norm_t(0, NPT, 0, 2 * GB)
         norm_v(2 * GB * NPT, B)
 
         for u in range(2):

@@ -346,19 +346,21 @@ def tile_haint_attention_t_kernel(tc, ht, ct, hi, W_as, W_ah, ba, v, W_a, out):
             rv = rden[:].rearrange("p (j b) -> p j b", j=4)
             nc.vector.reciprocal(out=rv[:, :, b0:b0 + n], in_=dv[:, :, b0:b0 + n])
 
-        def norm_t(c0, q, b0, nb):
-            w = 4 * nb
+        def norm(u):
+            bt = 2 * GB * NPT
+            nv, rv = [t[:].rearrange("p (j b) -> p j b", j=4)[:, 2 * u:2 * u + 2, :] for t in (num, rden)]
             nc.vector.tensor_tensor(
-                out=num[:].rearrange("p (j b) -> p j b", j=4)[:, :, b0:b0 + q * nb].rearrange(
-                    "p j (q b) -> p q j b", q=q),
-                in0=nps[:, c0:c0 + q * w].rearrange("p (q j b) -> p q j b", q=q, j=4),
-                in1=rden[:].rearrange("p (j b) -> p j b", j=4)[:, :, b0:b0 + q * nb].rearrange(
-                    "p j (q b) -> p q j b", q=q),
-                op=ALU.mult)
+                out=nv[:, :, 0:bt].rearrange("p j (q b) -> p q j b", q=NPT),
+                in0=nps[:, 0:4 * bt].rearrange("p (q j b) -> p q j b", q=NPT, j=4)[:, :, 2 * u:2 * u + 2, :],
+                in1=rv[:, :, 0:bt].rearrange("p j (q b) -> p q j b", q=NPT), op=ALU.mult)
+            nc.vector.tensor_tensor(out=nv[:, :, bt:B], in0=nv[:, :, bt:B], in1=rv[:, :, bt:B], op=ALU.mult)
 
-        def norm_v(b0, b1):
-            jb = [t[:].rearrange("p (j b) -> p j b", j=4)[:, :, b0:b1] for t in (num, rden)]
-            nc.vector.tensor_tensor(out=jb[0], in0=jb[0], in1=jb[1], op=ALU.mult)
+        def rs():
+            halves = [slice(2 * B * u, 2 * B * (u + 1)) for u in range(2)]
+            for c in halves:
+                nc.scalar.activation(out=rden[:, c], in_=den[:, c], func=ACTF.Abs_reciprocal_sqrt)
+            for c in halves:
+                nc.scalar.activation(out=rden[:, c], in_=rden[:, c], func=ACTF.Square)
 
         def rp(G, j0, j1):
             nc.vector.tensor_reduce(
@@ -413,8 +415,8 @@ def tile_haint_attention_t_kernel(tc, ht, ct, hi, W_as, W_ah, ba, v, W_a, out):
         nc.sync.dma_start(out=q_sb[:, 0:H], in_=ht)
         nc.sync.dma_start(out=q_sb[:, H:2 * H], in_=ct)
         nc.sync.dma_start(out=ba_t[0:8, :], in_=ba.rearrange("o (r c) -> (o r) c", r=8))
-        ldw(2, W_ah, 0)
         ldw(0, W_as[0:H, :], 1)
+        ldw(2, W_ah, 0)
         ldw(1, W_as[H:2 * H, :], 1)
         ldw(2, W_ah, 1)
         ld(1)
@@ -503,32 +505,32 @@ def tile_haint_attention_t_kernel(tc, ht, ct, hi, W_as, W_ah, ba, v, W_a, out):
         psb = ps_z.tile([P, P], BF16, name="psb", tag="psz")
         nc.tensor.transpose(psb[:], ba_t[:], ident_b[:])
         nc.vector.tensor_copy(out=ba_col[:], in_=psb[:, 0:8])
-        regroup(2, 0)
         qh(0)
+        regroup(0, 1)
         nc.vector.quantize_mx(out=q_codes[:].bitcast(FP8X4), scales=q_scales[:], in_=qg_t[:])
         bias_mm(0)
+        regroup(2, 0)
+        quantw(0, 1)
+        regroup(1, 1)
         quantw(2, 0)
         bias_add(0)
         s1(0, 0, 0)
         s1(0, 0, 1)
         s1(0, 0, 2)
-        regroup(0, 1)
         regroup(2, 1)
-        regroup(1, 1)
         tr(1, 0)
         ev(1, 0)
         tr(1, 1)
+        quantw(1, 1)
         add(0, 0, 0)
         s1(0, 0, 3)
-        quantw(0, 1)
         add(0, 0, 1)
-        quantw(1, 1)
         bias_mm(1)
         tanh(0, 0, 0)
         add(0, 0, 2)
         ev(1, 1)
-        add(0, 0, 3)
         quantw(2, 1)
+        add(0, 0, 3)
         bias_add(1)
         tanh(0, 0, 1)
         wa_regroup(0, 0)
@@ -631,12 +633,12 @@ def tile_haint_attention_t_kernel(tc, ht, ct, hi, W_as, W_ah, ba, v, W_a, out):
         add(G, 1, 0)
         add(G, 1, 1)
         add(G, 1, 2)
+        mx(G - 1, 1)
         tok(prs[G - 2][:, 2 * GB * T:2 * GB * T + 1], tok_g(0, G))
         qg(G, 0)
         mul(G - 2, 2, 4)
         tanh(G, 1, 0)
         tanh(G, 1, 1)
-        mx(G - 1, 1)
         sm(3, 3, 4)
         s2(G - 1, 3)
         ex(G - 1, 1)
@@ -654,6 +656,7 @@ def tile_haint_attention_t_kernel(tc, ht, ct, hi, W_as, W_ah, ba, v, W_a, out):
         s2(G, 2)
         s2(G, 3)
         sm(3, 7, 10)
+        rp(G - 2, 0, 2)
         mx(G, 0)
         ex(G, 0)
         mx(G, 1)
@@ -661,24 +664,22 @@ def tile_haint_attention_t_kernel(tc, ht, ct, hi, W_as, W_ah, ba, v, W_a, out):
         mx(G, 2)
         ex(G, 2)
         mul(G - 1, 2, 4)
-        rp(G - 2, 0, 2)
         mx(G, 3)
         ex(G, 3)
+        rs()
         rp(G - 2, 2, 4)
         rp(G - 1, 0, 2)
-        nc.scalar.activation(out=rden[:], in_=den[:], func=ACTF.Abs_reciprocal_sqrt)
-        nc.scalar.activation(out=rden[:], in_=rden[:], func=ACTF.Square)
         dmm(G, 0, nc.gpsimd)
         rp(G - 1, 2, 4)
         dmm(G, 1, nc.vector)
-        dmm(G, 2, nc.vector)
-        dmm(G, 3, nc.vector)
         dms(G, 0)
+        dmm(G, 2, nc.vector)
         dms(G, 1)
+        dmm(G, 3, nc.vector)
         dms(G, 2)
+        norm(0)
         dms(G, 3)
-        norm_t(0, NPT, 0, 2 * GB)
-        norm_v(2 * GB * NPT, B)
+        norm(1)
 
         for u in range(2):
             ps = ps_z.tile([P, 2 * P], F32, name="pso", tag="psz")

@@ -28,7 +28,7 @@ N_HS = 3
 N_GQ = 3
 N_HIT = 5
 NPT = 4
-EV_S = (0, 1)
+EV_S = [(0, 0), (0, 1), (1, 0), (1, 1), (2, 1)]
 
 
 def tile_haint_attention_t_kernel(tc, ht, ct, hi, W_as, W_ah, ba, v, W_a, out):
@@ -147,7 +147,7 @@ def tile_haint_attention_t_kernel(tc, ht, ct, hi, W_as, W_ah, ba, v, W_a, out):
             dst = hit[G][:].bitcast(F32)[:, wp * 512:(wp + 1) * 512].rearrange(
                 "p (w c u) -> p w c u", w=2, c=P, u=2)[:, :, 0:WR, :]
             srcv = tps[(G, wp)][:].rearrange("p (w u c) -> p w c u", w=2, u=2, c=P)[:, :, 0:WR, :]
-            if G in EV_S:
+            if (G, wp) in EV_S:
                 nc.scalar.copy(out=dst, in_=srcv)
             else:
                 nc.vector.tensor_copy(out=dst, in_=srcv)
@@ -548,6 +548,7 @@ def tile_haint_attention_t_kernel(tc, ht, ct, hi, W_as, W_ah, ba, v, W_a, out):
                 add(G, 0, 1)
                 s1(G, 0, 3)
                 tanh(G, 0, 0)
+                ev(G + 1, 1)
                 wa_quant(1)
             if G > 0:
                 s2(G - 1, 0)
@@ -576,7 +577,6 @@ def tile_haint_attention_t_kernel(tc, ht, ct, hi, W_as, W_ah, ba, v, W_a, out):
             mx(G - 1, 0)
             ex(G - 1, 0)
             if G == 1:
-                ev(G + 1, 1)
                 qh(G + 1)
             s1(G, 1, 2)
             add(G, 1, 0)
@@ -613,12 +613,12 @@ def tile_haint_attention_t_kernel(tc, ht, ct, hi, W_as, W_ah, ba, v, W_a, out):
         G = NG - 1
         add(G, 0, 0)
         s1(G, 1, 0)
+        add(G, 0, 1)
+        s1(G, 1, 1)
         a10_tok(G - 3, tok_g(1, G - 1))
         qg(G - 1, 1)
         a10(G - 3)
         s2(G - 1, 0)
-        add(G, 0, 1)
-        s1(G, 1, 1)
         s2(G - 1, 1)
         tanh(G, 0, 0)
         add(G, 0, 2)
@@ -645,6 +645,7 @@ def tile_haint_attention_t_kernel(tc, ht, ct, hi, W_as, W_ah, ba, v, W_a, out):
         mx(G - 1, 2)
         ex(G - 1, 2)
         sm(3, 4, 7)
+        rp(G - 2, 0, 2)
         mx(G - 1, 3)
         ex(G - 1, 3)
         prs[G - 1] = prp.tile([P, 4 * GB * T], F32, name="pr", tag="pr")
@@ -656,29 +657,30 @@ def tile_haint_attention_t_kernel(tc, ht, ct, hi, W_as, W_ah, ba, v, W_a, out):
         s2(G, 2)
         s2(G, 3)
         sm(3, 7, 10)
-        rp(G - 2, 0, 2)
+        rp(G - 2, 2, 4)
         mx(G, 0)
         ex(G, 0)
         mx(G, 1)
         ex(G, 1)
         mx(G, 2)
         ex(G, 2)
-        mul(G - 1, 2, 4)
+        mul(G - 1, 2, 3)
+        mul(G - 1, 3, 4)
         mx(G, 3)
         ex(G, 3)
         rs()
-        rp(G - 2, 2, 4)
         rp(G - 1, 0, 2)
+        rp(G - 1, 2, 3)
         dmm(G, 0, nc.gpsimd)
-        rp(G - 1, 2, 4)
+        rp(G - 1, 3, 4)
         dmm(G, 1, nc.vector)
         dms(G, 0)
         dmm(G, 2, nc.vector)
         dms(G, 1)
         dmm(G, 3, nc.vector)
         dms(G, 2)
-        norm(0)
         dms(G, 3)
+        norm(0)
         norm(1)
 
         for u in range(2):

from contextlib import ExitStack

import concourse.mybir as mybir
from concourse.masks import make_identity

F32 = mybir.dt.float32
BF16 = mybir.dt.bfloat16
U32 = mybir.dt.uint32
U8 = mybir.dt.uint8
FP8X4 = mybir.dt.float8_e4m3fn_x4
ACTF = mybir.ActivationFunctionType
ALU = mybir.AluOpType
AX = mybir.AxisListType

P = 128
B, T, H, A = 128, 40, 512, 1024
FLOPS = 2 * B * (2 * H) * A + 2 * B * T * H * A + 2 * B * T * A * H

WB = 3
WR = WB * T
WIN = 128
GW = 4
GB = WB * GW
NG = 11
HW = 512
CS = (256, 224)
N_HS = 3
N_GQ = 3
N_HIT = 5
NPT = 4
EV_S = [(0, 0), (0, 1), (1, 0), (1, 1), (2, 1)]


def tile_haint_attention_t_kernel(tc, ht, ct, hi, W_as, W_ah, ba, v, W_a, out):
    nc = tc.nc
    with ExitStack() as ctx:
        const = ctx.enter_context(tc.tile_pool(name="const", bufs=1))
        wraw = ctx.enter_context(tc.tile_pool(name="wraw", bufs=6))
        wgrp = ctx.enter_context(tc.tile_pool(name="wgrp", bufs=3))
        warp = ctx.enter_context(tc.tile_pool(name="warp", bufs=1))
        hicp = ctx.enter_context(tc.tile_pool(name="hicp", bufs=3))
        xpool = ctx.enter_context(tc.tile_pool(name="xpool", bufs=4))
        gcp = ctx.enter_context(tc.tile_pool(name="gcp", bufs=6))
        epool = ctx.enter_context(tc.tile_pool(name="epool", bufs=2))
        prp = ctx.enter_context(tc.tile_pool(name="prp", bufs=2))
        qrp = ctx.enter_context(tc.tile_pool(name="qrp", bufs=2))
        rrp = ctx.enter_context(tc.tile_pool(name="rrp", bufs=2))
        small = ctx.enter_context(tc.tile_pool(name="small", bufs=8))
        ps_t = ctx.enter_context(tc.psum_pool(name="ps_t", bufs=1))
        ps_n = ctx.enter_context(tc.psum_pool(name="ps_n", bufs=1))
        ps_1 = ctx.enter_context(tc.psum_pool(name="ps_1", bufs=3))
        ps_z = ctx.enter_context(tc.psum_pool(name="ps_z", bufs=3))

        def nb_of(G, w):
            return max(0, min(WB, B - (GB * G + WB * w)))

        def segs_of(G):
            segs = []
            for w in range(GW):
                n = nb_of(G, w)
                if n == 0:
                    continue
                if segs and segs[-1][2] == n:
                    segs[-1] = (segs[-1][0], segs[-1][1] + 1, n)
                else:
                    segs.append((w, 1, n))
            return segs

        ident_f = const.tile([P, P], F32, name="ident_f")
        make_identity(nc, ident_f[:])
        ident_b = const.tile([P, P], BF16, name="ident_b")
        make_identity(nc, ident_b[:])

        hs = [const.tile([P, GW * H], BF16, name="hs%d" % i) for i in range(N_HS)]
        ba_t = const.tile([P, P], BF16, name="ba_t")
        gq = [[const.tile([P, GW * WIN * 4], BF16, name="gq%d_%d" % (i, c), align_bytes=64)
               for c in range(2)] for i in range(N_GQ)]
        hits = [const.tile([P, GW * WIN * 4], BF16, name="hit%d" % i, align_bytes=64)
                for i in range(N_HIT)]
        q_sb = const.tile([P, 2 * H], BF16, name="q_sb")
        qg_t = const.tile([P, 2 * P * 4], BF16, name="qg_t", align_bytes=64)
        q_codes = const.tile([P, 2 * P], U32, name="q_codes", align_bytes=64)
        q_scales = const.tile([P, 2 * P], U8, name="q_scales", align_bytes=64)
        as_codes = const.tile([P, 2 * A], U32, name="as_codes", align_bytes=64)
        as_scales = const.tile([P, 2 * A], U8, name="as_scales", align_bytes=64)
        ah_codes = const.tile([P, A], U32, name="ah_codes", align_bytes=64)
        ah_scales = const.tile([P, A], U8, name="ah_scales", align_bytes=64)
        a_codes = const.tile([P, 2 * H], U32, name="a_codes", align_bytes=64)
        a_scales = const.tile([P, 2 * H], U8, name="a_scales", align_bytes=64)
        c_sb = const.tile([P, 2 * B * 4], F32, name="c_sb")
        warm = const.tile([P, 1], F32, name="warm")
        ba_col = const.tile([P, 8], F32, name="ba_col")
        den = const.tile([P, 4 * B], F32, name="den")
        num = const.tile([P, 4 * B], F32, name="num")
        rden = const.tile([P, 4 * B], F32, name="rden")
        out_sb = const.tile([P, H], F32, name="out_sb")

        hi_rows = hi.rearrange("b t h -> (b t) h")
        hit = {}
        hic = {}
        tps = {}
        ps1s = {}
        xs = {}
        gcs = {}
        pszs = {}
        negms = {}
        es = {}
        prs = {}
        qrs = {}
        rrs = {}

        ctx.enter_context(tc.manual_schedule())

        nps = ps_n.tile([P, 512], F32, name="nps")

        def ld(G):
            if G >= NG:
                return
            dst = hs[G % N_HS]
            for w in range(GW):
                r0 = (GW * G + w) * WR
                n = min(P, B * T - r0)
                if n > 0:
                    nc.sync.dma_start(out=dst[0:n, w * H:(w + 1) * H], in_=hi_rows[r0:r0 + n, :])

        def tr(G, wp):
            if G >= NG:
                return
            src = hs[G % N_HS]
            if G < 2 and wp == 1:
                tp = ps_z.tile([P, 512], F32, name="tp1", tag="psz")
            else:
                tp = ps_t.tile([P, 512], F32, name="tp", tag="tp")
            for wl in range(2):
                w = 2 * wp + wl
                for u in range(2):
                    nc.tensor.transpose(
                        tp[:, (2 * wl + u) * P:(2 * wl + u + 1) * P],
                        src[:, w * H:(w + 1) * H].bitcast(F32)[:, u * P:(u + 1) * P],
                        ident_f[:])
            tps[(G, wp)] = tp

        def ev(G, wp):
            if G >= NG:
                return
            hit[G] = hits[G % N_HIT]
            dst = hit[G][:].bitcast(F32)[:, wp * 512:(wp + 1) * 512].rearrange(
                "p (w c u) -> p w c u", w=2, c=P, u=2)[:, :, 0:WR, :]
            srcv = tps[(G, wp)][:].rearrange("p (w u c) -> p w c u", w=2, u=2, c=P)[:, :, 0:WR, :]
            if (G, wp) in EV_S:
                nc.scalar.copy(out=dst, in_=srcv)
            else:
                nc.vector.tensor_copy(out=dst, in_=srcv)

        def qh(G):
            if G >= NG:
                return
            codes = hicp.tile([P, GW * WIN], U32, name="hic", tag="hic", align_bytes=64)
            scales = hicp.tile([P, GW * WIN], U8, name="his", tag="his", align_bytes=64)
            nc.vector.quantize_mx(out=codes[:].bitcast(FP8X4), scales=scales[:], in_=hit[G][:])
            hic[G] = (codes, scales)

        def s1(G, c, w):
            if G >= NG or nb_of(G, w) == 0:
                return
            codes, scales = hic[G]
            ps1 = ps_1.tile([P, 512], F32, name="ps1", tag="ps1")
            for j in range(4):
                m = 4 * c + j
                nc.tensor.matmul_mx(
                    out=ps1[:, j * P:(j + 1) * P],
                    lhsT=ah_codes[:, m * P:(m + 1) * P].bitcast(FP8X4),
                    lhsT_scale=ah_scales[:, m * P:(m + 1) * P],
                    rhs=codes[:, w * WIN:(w + 1) * WIN].bitcast(FP8X4),
                    rhs_scale=scales[:, w * WIN:(w + 1) * WIN],
                    start=True, stop=True)
            ps1s[(G, c, w)] = ps1

        def add(G, c, w):
            if G >= NG or nb_of(G, w) == 0:
                return
            n = nb_of(G, w)
            b0 = GB * G + WB * w
            if w % 2 == 0:
                xs[(G, c, w // 2)] = xpool.tile([P, 2 * WR * 4], F32, name="x", tag="x")
            x = xs[(G, c, w // 2)]
            x0 = (w % 2) * WR * 4
            nc.vector.tensor_tensor(
                out=x[:, x0:x0 + n * T * 4].rearrange("p (b t j) -> p b t j", b=n, t=T, j=4),
                in0=ps1s[(G, c, w)][:].rearrange("p (j r) -> p j r", j=4)[:, :, 0:n * T].rearrange(
                    "p j (b t) -> p b t j", b=n),
                in1=c_sb[:, c * 512 + 4 * b0:c * 512 + 4 * (b0 + n)].rearrange(
                    "p (b j) -> p b j", j=4).unsqueeze(2).to_broadcast([P, n, T, 4]),
                op=ALU.add)

        def tanh(G, c, wp):
            if G >= NG:
                return
            ws = [w for w in (2 * wp, 2 * wp + 1) if nb_of(G, w) > 0]
            if not ws:
                return
            x = xs[(G, c, wp)]
            gv = gq[G % N_GQ][c][:].rearrange("p (w y) -> p w y", w=GW)
            if all(nb_of(G, w) == WB for w in ws):
                nw = len(ws)
                nc.scalar.activation(
                    out=gv[:, ws[0]:ws[0] + nw, 0:WR * 4],
                    in_=x[:, 0:nw * WR * 4].rearrange("p (w y) -> p w y", w=nw),
                    func=ACTF.Tanh)
            else:
                for w in ws:
                    n = nb_of(G, w)
                    x0 = (w % 2) * WR * 4
                    nc.scalar.activation(out=gv[:, w, 0:n * T * 4],
                                         in_=x[:, x0:x0 + n * T * 4], func=ACTF.Tanh)

        def qg(G, c):
            if G < 0 or G >= NG:
                return
            gc = gcp.tile([P, GW * WIN], U32, name="gc", tag="gc", align_bytes=64)
            gs = gcp.tile([P, GW * WIN], U8, name="gs", tag="gs", align_bytes=64)
            nc.vector.quantize_mx(out=gc[:].bitcast(FP8X4), scales=gs[:],
                                  in_=gq[G % N_GQ][c][:])
            gcs[(G, c)] = (gc, gs)

        def s2(G, jj):
            if G < 0:
                return
            if G == NG - 1 and jj < 3:
                psz = ps_1.tile([P, 512], F32, name="psl", tag="ps1")
            else:
                psz = ps_z.tile([P, 512], F32, name="psz", tag="psz")
            for c in range(2):
                nc.tensor.matmul_mx(
                    out=psz[:],
                    lhsT=a_codes[:, c * H + jj * P:c * H + (jj + 1) * P].bitcast(FP8X4),
                    lhsT_scale=a_scales[:, c * H + jj * P:c * H + (jj + 1) * P],
                    rhs=gcs[(G, c)][0][:].bitcast(FP8X4), rhs_scale=gcs[(G, c)][1][:],
                    start=(c == 0), stop=(c == 1))
            pszs[(G, jj)] = psz

        def mx(G, jj):
            if G < 0:
                return
            zv = pszs[(G, jj)][:].rearrange("p (w c) -> p w c", w=GW)
            negm = small.tile([P, GB], F32, name="negm", tag="negm")
            nw = sum(1 for w in range(GW) if nb_of(G, w) > 0)
            nc.vector.tensor_reduce(
                out=negm[:, 0:WB * nw].rearrange("p (w b) -> p w b", w=nw),
                in_=zv[:, 0:nw, 0:WR].rearrange("p w (b t) -> p w b t", b=WB),
                axis=AX.X, op=ALU.max, negate=True)
            negms[(G, jj)] = negm

        def ex(G, jj):
            if G < 0:
                return
            if jj == 0:
                es[G] = epool.tile([P, 4 * GB * T], F32, name="e", tag="e")
            e = es[G]
            psz = pszs[(G, jj)]
            negm = negms[(G, jj)]
            nbg = sum(nb_of(G, w) for w in range(GW))
            for k in range(nbg):
                w, b3 = divmod(k, WB)
                col = jj * B + GB * G + k
                nc.scalar.activation(
                    out=e[:, (jj * GB + k) * T:(jj * GB + k + 1) * T],
                    in_=psz[:, w * WIN + b3 * T:w * WIN + (b3 + 1) * T],
                    func=ACTF.Exp, bias=negm[:, k:k + 1], scale=1.0,
                    accum_out=den[:, col:col + 1])

        def tok(dst, src):
            nc.vector.tensor_copy(out=dst, in_=src)

        def tok_g(c, G):
            w = GW - 1
            while nb_of(G, w) == 0:
                w -= 1
            return gq[G % N_GQ][c][:].rearrange("p (w y) -> p w y", w=GW)[:, w, 0:1]

        def mul_tok(G, src):
            if G < 0:
                return
            prs[G] = prp.tile([P, 4 * GB * T], F32, name="pr", tag="pr")
            tok(prs[G][:, 0:1], src)

        def mul(G, h0=0, h1=4):
            if G < 0:
                return
            if G not in prs:
                prs[G] = prp.tile([P, 4 * GB * T], F32, name="pr", tag="pr")
            hv = hit[G][:].rearrange("p (w c t) -> p t w c", w=GW, c=WIN, t=4)
            nc.gpsimd.tensor_tensor(
                out=prs[G][:].rearrange("p (j w r) -> p j w r", j=4, w=GW)[:, h0:h1, :, :],
                in0=es[G][:].rearrange("p (j w r) -> p j w r", j=4, w=GW)[:, h0:h1, :, :],
                in1=hv[:, h0:h1, :, 0:WR], op=ALU.mult)

        def a20_tok(G, src):
            if G < 0:
                return
            qrs[G] = qrp.tile([P, 4 * GB * 20], F32, name="qr", tag="qr")
            tok(qrs[G][:, 0:1], src)

        def a20(G):
            if G < 0:
                return
            pv = prs[G][:].rearrange("p (x t) -> p x t", t=T)
            nc.gpsimd.tensor_tensor(out=qrs[G][:].rearrange("p (x t) -> p x t", t=20),
                                    in0=pv[:, :, 0:20], in1=pv[:, :, 20:40], op=ALU.add)

        def a10_tok(G, src):
            if G < 0:
                return
            if G % 2 == 0:
                rrs[G // 2] = rrp.tile([P, 8 * GB * 10], F32, name="rr", tag="rr")
            g0 = (G % 2) * GB * 10
            tok(rrs[G // 2][:, g0:g0 + 1], src)

        def a10(G):
            if G < 0:
                return
            qv = qrs[G][:].rearrange("p (j b t) -> p j b t", j=4, t=20)
            rv = rrs[G // 2][:].rearrange("p (j g b t) -> p j g b t", j=4, g=2, t=10)[:, :, G % 2, :, :]
            nc.gpsimd.tensor_tensor(out=rv, in0=qv[:, :, :, 0:10], in1=qv[:, :, :, 10:20], op=ALU.add)

        def sm(p, i0, i1):
            if p < 0 or p >= NPT:
                return
            rp_ = rrs[p][:].rearrange("p (x t) -> p t x", t=10)
            for i in range(i0, i1):
                nc.tensor.matmul(nps[:, 8 * GB * p:8 * GB * (p + 1)], lhsT=ident_f[:], rhs=rp_[:, i, :],
                                 start=(i == 0), stop=(i == 9))

        def sm1(G, i0, i1):
            q1 = prs[G][:].rearrange("p (x t) -> p t x", t=T)
            for i in range(i0, i1):
                nc.tensor.matmul(nps[:, 4 * GB * G:4 * GB * G + 2 * GB], lhsT=ident_f[:],
                                 rhs=q1[:, i, 0:2 * GB], start=(i == 0), stop=(i == T - 1))

        def rc(G):
            if G < 0:
                return
            b0 = GB * G
            n = sum(nb_of(G, w) for w in range(GW))
            dv = den[:].rearrange("p (j b) -> p j b", j=4)
            rv = rden[:].rearrange("p (j b) -> p j b", j=4)
            nc.vector.reciprocal(out=rv[:, :, b0:b0 + n], in_=dv[:, :, b0:b0 + n])

        def norm(u):
            bt = 2 * GB * NPT
            nv, rv = [t[:].rearrange("p (j b) -> p j b", j=4)[:, 2 * u:2 * u + 2, :] for t in (num, rden)]
            nc.vector.tensor_tensor(
                out=nv[:, :, 0:bt].rearrange("p j (q b) -> p q j b", q=NPT),
                in0=nps[:, 0:4 * bt].rearrange("p (q j b) -> p q j b", q=NPT, j=4)[:, :, 2 * u:2 * u + 2, :],
                in1=rv[:, :, 0:bt].rearrange("p j (q b) -> p q j b", q=NPT), op=ALU.mult)
            nc.vector.tensor_tensor(out=nv[:, :, bt:B], in0=nv[:, :, bt:B], in1=rv[:, :, bt:B], op=ALU.mult)

        def rs():
            halves = [slice(2 * B * u, 2 * B * (u + 1)) for u in range(2)]
            for c in halves:
                nc.scalar.activation(out=rden[:, c], in_=den[:, c], func=ACTF.Abs_reciprocal_sqrt)
            for c in halves:
                nc.scalar.activation(out=rden[:, c], in_=rden[:, c], func=ACTF.Square)

        def rp(G, j0, j1):
            nc.vector.tensor_reduce(
                out=num[:].rearrange("p (j b) -> p j b", j=4)[:, j0:j1, GB * G:GB * G + GB],
                in_=prs[G][:].rearrange("p (j b t) -> p j b t", j=4, b=GB)[:, j0:j1, :, :],
                axis=AX.X, op=ALU.add)

        def dmm(G, jj, eng):
            hv = hit[G][:].rearrange("p (w c t) -> p w c t", w=GW, c=WIN, t=4)
            for (w0, nw, n) in segs_of(G):
                e0 = jj * GB * T + WR * w0
                evw = es[G][:, e0:e0 + nw * n * T].rearrange("p (w r) -> p w r", w=nw)
                eng.tensor_tensor(out=evw, in0=evw, in1=hv[:, w0:w0 + nw, 0:n * T, jj], op=ALU.mult)

        def dmsS(G, jj, src):
            nbg = sum(nb_of(G, w) for w in range(GW))
            for k in range(nbg):
                v = src[:, (jj * GB + k) * T:(jj * GB + k + 1) * T]
                c0 = jj * B + GB * G + k
                nc.scalar.activation(out=v, in_=v, func=ACTF.Copy, accum_out=num[:, c0:c0 + 1])

        def dms(G, jj):
            nbg = sum(nb_of(G, w) for w in range(GW))
            c0 = jj * B + GB * G
            nc.vector.tensor_reduce(
                out=num[:, c0:c0 + nbg],
                in_=es[G][:, jj * GB * T:jj * GB * T + nbg * T].rearrange("p (b t) -> p b t", t=T),
                axis=AX.X, op=ALU.add)

        nc.gpsimd.memset(ba_t[:], 0.0)
        for t in hits + [t for pair in gq for t in pair]:
            nc.gpsimd.memset(
                t[:].rearrange("p (w y) -> p w y", w=GW)[:, :, WR * 4:WIN * 4], 0.0)

        nc.vector.memset(warm[:], 0.0)
        nc.scalar.activation(out=warm[:], in_=warm[:], func=ACTF.Tanh)

        raw = {}

        def ldw(name, src, h):
            r = wraw.tile([P, 4 * HW], BF16, name="wr", tag="wr")
            for u in range(2):
                nc.sync.dma_start(
                    out=r[:].rearrange("p (u e a) -> p u e a", u=2, e=2)[:, u, :, :],
                    in_=src[2 * P * u:2 * P * (u + 1), h * HW:(h + 1) * HW].rearrange(
                        "(p e) a -> p e a", e=2))
            raw[(name, h)] = r

        ldw(0, W_as[0:H, :], 0)
        ldw(1, W_as[H:2 * H, :], 0)
        ld(0)
        nc.sync.dma_start(out=q_sb[:, 0:H], in_=ht)
        nc.sync.dma_start(out=q_sb[:, H:2 * H], in_=ct)
        nc.sync.dma_start(out=ba_t[0:8, :], in_=ba.rearrange("o (r c) -> (o r) c", r=8))
        ldw(0, W_as[0:H, :], 1)
        ldw(2, W_ah, 0)
        ldw(1, W_as[H:2 * H, :], 1)
        ldw(2, W_ah, 1)
        ld(1)
        a_raw = warp.tile([P, 8 * H], BF16, name="a_raw")
        nc.sync.dma_start(out=a_raw[:].rearrange("p (r h) -> p r h", r=8),
                          in_=W_a.rearrange("(r p) h -> p r h", p=P))
        ld(2)

        grp = {}
        wcodes = {0: as_codes[:, 0:A], 1: as_codes[:, A:2 * A], 2: ah_codes[:]}
        wscales = {0: as_scales[:, 0:A], 1: as_scales[:, A:2 * A], 2: ah_scales[:]}

        def regroup(name, h):
            g = wgrp.tile([P, 4 * HW], BF16, name="wg", tag="wg", align_bytes=64)
            s = raw[(name, h)][:].rearrange("p (t a) -> p t a", t=4)
            d = g[:].rearrange("p (a t) -> p a t", t=4)
            cs = CS[h]
            nc.vector.tensor_copy(
                out=d[:, 0:cs, :].rearrange("p (c i) t -> p c t i", i=4),
                in_=s[:, :, 0:cs].rearrange("p t (c i) -> p c t i", i=4))
            nc.scalar.copy(
                out=d[:, cs:HW, :].rearrange("p (c i) t -> p c t i", i=4),
                in_=s[:, :, cs:HW].rearrange("p t (c i) -> p c t i", i=4))
            grp[(name, h)] = g

        def quantw(name, h):
            nc.vector.quantize_mx(out=wcodes[name][:, h * HW:(h + 1) * HW].bitcast(FP8X4),
                                  scales=wscales[name][:, h * HW:(h + 1) * HW],
                                  in_=grp[(name, h)][:])

        def bias_mm(c):
            ps0 = ps_1.tile([P, 512], F32, name="ps0", tag="ps1")
            for j in range(4):
                m = 4 * c + j
                for g in range(2):
                    nc.tensor.matmul_mx(
                        out=ps0[:, j * P:(j + 1) * P],
                        lhsT=as_codes[:, g * A + m * P:g * A + (m + 1) * P].bitcast(FP8X4),
                        lhsT_scale=as_scales[:, g * A + m * P:g * A + (m + 1) * P],
                        rhs=q_codes[:, g * P:(g + 1) * P].bitcast(FP8X4),
                        rhs_scale=q_scales[:, g * P:(g + 1) * P],
                        start=(g == 0), stop=(g == 1))
            ps0s[c] = ps0

        def bias_add(c):
            nc.vector.tensor_tensor(
                out=c_sb[:, c * 512:(c + 1) * 512].rearrange("p (b j) -> p b j", j=4),
                in0=ps0s[c][:].rearrange("p (j b) -> p b j", j=4),
                in1=ba_col[:, 4 * c:4 * c + 4].unsqueeze(1).to_broadcast([P, B, 4]),
                op=ALU.add)

        a_grp = warp.tile([P, 4 * A], BF16, name="a_grp", align_bytes=64)

        def wa_regroup(c, u):
            o0 = c * 2048 + u * 1024
            dst = a_grp[:, o0:o0 + 1024].rearrange("p (e q t) -> p e q t", e=2, q=P, t=4)
            wsrc = a_raw[:].rearrange("p (r h) -> p r h", r=8)[
                :, 4 * c:4 * c + 4, 256 * u:256 * (u + 1)].rearrange("p t (q e) -> p e q t", e=2)
            if (c, u) == (0, 1):
                nc.gpsimd.tensor_scalar(out=dst, in0=wsrc, scalar1=1.0, scalar2=0.0,
                                        op0=ALU.mult, op1=ALU.add)
            else:
                nc.scalar.copy(out=dst, in_=wsrc)

        def wa_quant(c):
            nc.vector.quantize_mx(out=a_codes[:, c * H:(c + 1) * H].bitcast(FP8X4),
                                  scales=a_scales[:, c * H:(c + 1) * H],
                                  in_=a_grp[:, c * 2048:(c + 1) * 2048])

        ps0s = {}
        regroup(0, 0)
        regroup(1, 0)
        quantw(0, 0)
        tr(0, 0)
        ev(0, 0)
        tr(0, 1)
        tq = ps_z.tile([P, 512], F32, name="tq", tag="psz")
        for gu in range(4):
            nc.tensor.transpose(tq[:, gu * P:(gu + 1) * P],
                                q_sb[:].bitcast(F32)[:, gu * P:(gu + 1) * P], ident_f[:])
        quantw(1, 0)
        ev(0, 1)
        nc.scalar.copy(
            out=qg_t[:].bitcast(F32).rearrange("p (g b u) -> p g b u", g=2, b=P, u=2),
            in_=tq[:].rearrange("p (g u b) -> p g b u", g=2, u=2, b=P))
        psb = ps_z.tile([P, P], BF16, name="psb", tag="psz")
        nc.tensor.transpose(psb[:], ba_t[:], ident_b[:])
        nc.vector.tensor_copy(out=ba_col[:], in_=psb[:, 0:8])
        qh(0)
        regroup(0, 1)
        nc.vector.quantize_mx(out=q_codes[:].bitcast(FP8X4), scales=q_scales[:], in_=qg_t[:])
        bias_mm(0)
        regroup(2, 0)
        quantw(0, 1)
        regroup(1, 1)
        quantw(2, 0)
        bias_add(0)
        s1(0, 0, 0)
        s1(0, 0, 1)
        s1(0, 0, 2)
        regroup(2, 1)
        tr(1, 0)
        ev(1, 0)
        tr(1, 1)
        quantw(1, 1)
        add(0, 0, 0)
        s1(0, 0, 3)
        add(0, 0, 1)
        bias_mm(1)
        tanh(0, 0, 0)
        add(0, 0, 2)
        ev(1, 1)
        quantw(2, 1)
        add(0, 0, 3)
        bias_add(1)
        tanh(0, 0, 1)
        wa_regroup(0, 0)
        for G in range(NG - 1):
            sp = (G - 4) // 2
            si = 5 * (G % 2)
            ld(G + 3)
            if G > 0:
                a10_tok(G - 3, tok_g(1, G - 1))
                qg(G - 1, 1)
                a10(G - 3)
                add(G, 0, 0)
            if G == 1:
                wa_quant(0)
                add(G, 0, 1)
                s1(G, 0, 3)
                tanh(G, 0, 0)
                ev(G + 1, 1)
                wa_quant(1)
            if G > 0:
                s2(G - 1, 0)
            if G > 1:
                s1(G, 0, 3)
            if G > 0:
                s2(G - 1, 1)
            if G > 1:
                add(G, 0, 1)
                tanh(G, 0, 0)
            s1(G, 1, 0)
            if G == 0:
                tok(a_grp[:, 1024:1025], hit[1][:, 2 * WIN * 4:2 * WIN * 4 + 1])
            if G != 1:
                qh(G + 1)
                mul(G - 2)
            if G == 0:
                wa_regroup(0, 1)
            s2(G - 1, 2)
            if G > 0:
                add(G, 0, 2)
                add(G, 0, 3)
                tanh(G, 0, 1)
            s1(G, 1, 1)
            sm(sp, si, si + 1)
            mx(G - 1, 0)
            ex(G - 1, 0)
            if G == 1:
                qh(G + 1)
            s1(G, 1, 2)
            add(G, 1, 0)
            s1(G, 1, 3)
            tr(G + 2, 0)
            sm(sp, si + 1, si + 2)
            add(G, 1, 1)
            tanh(G, 1, 0)
            mx(G - 1, 1)
            s1(G + 1, 0, 0)
            sm(sp, si + 2, si + 3)
            add(G, 1, 2)
            s2(G - 1, 3)
            s1(G + 1, 0, 1)
            add(G, 1, 3)
            tanh(G, 1, 1)
            if G == 0:
                wa_regroup(1, 0)
                wa_regroup(1, 1)
            ex(G - 1, 1)
            a20_tok(G - 2, tok_g(0, G))
            qg(G, 0)
            a20(G - 2)
            ev(G + 2, 0)
            s1(G + 1, 0, 2)
            tr(G + 2, 1)
            sm(sp, si + 3, si + 5)
            mx(G - 1, 2)
            ex(G - 1, 2)
            mx(G - 1, 3)
            ex(G - 1, 3)
            if G > 0:
                ev(G + 2, 1)
        G = NG - 1
        add(G, 0, 0)
        s1(G, 1, 0)
        add(G, 0, 1)
        s1(G, 1, 1)
        a10_tok(G - 3, tok_g(1, G - 1))
        qg(G - 1, 1)
        a10(G - 3)
        s2(G - 1, 0)
        s2(G - 1, 1)
        tanh(G, 0, 0)
        add(G, 0, 2)
        s1(G, 1, 2)
        tanh(G, 0, 1)
        s2(G - 1, 2)
        sm(3, 0, 3)
        mul_tok(G - 2, gq[(G - 1) % N_GQ][1][:, 0:1])
        mul(G - 2, 0, 2)
        mx(G - 1, 0)
        ex(G - 1, 0)
        add(G, 1, 0)
        add(G, 1, 1)
        add(G, 1, 2)
        mx(G - 1, 1)
        tok(prs[G - 2][:, 2 * GB * T:2 * GB * T + 1], tok_g(0, G))
        qg(G, 0)
        mul(G - 2, 2, 4)
        tanh(G, 1, 0)
        tanh(G, 1, 1)
        sm(3, 3, 4)
        s2(G - 1, 3)
        ex(G - 1, 1)
        mx(G - 1, 2)
        ex(G - 1, 2)
        sm(3, 4, 7)
        rp(G - 2, 0, 2)
        mx(G - 1, 3)
        ex(G - 1, 3)
        prs[G - 1] = prp.tile([P, 4 * GB * T], F32, name="pr", tag="pr")
        tok(prs[G - 1][:, 0:1], tok_g(1, G))
        qg(G, 1)
        mul(G - 1, 0, 2)
        s2(G, 0)
        s2(G, 1)
        s2(G, 2)
        s2(G, 3)
        sm(3, 7, 10)
        rp(G - 2, 2, 4)
        mx(G, 0)
        ex(G, 0)
        mx(G, 1)
        ex(G, 1)
        mx(G, 2)
        ex(G, 2)
        mul(G - 1, 2, 3)
        mul(G - 1, 3, 4)
        mx(G, 3)
        ex(G, 3)
        rs()
        rp(G - 1, 0, 2)
        rp(G - 1, 2, 3)
        dmm(G, 0, nc.gpsimd)
        rp(G - 1, 3, 4)
        dmm(G, 1, nc.vector)
        dms(G, 0)
        dmm(G, 2, nc.vector)
        dms(G, 1)
        dmm(G, 3, nc.vector)
        dms(G, 2)
        dms(G, 3)
        norm(0)
        norm(1)

        for u in range(2):
            ps = ps_z.tile([P, 2 * P], F32, name="pso", tag="psz")
            for e in range(2):
                jj = 2 * u + e
                nc.tensor.transpose(ps[:, e * P:(e + 1) * P], num[:, jj * P:(jj + 1) * P], ident_f[:])
            ov = out_sb[:, 2 * P * u:2 * P * (u + 1)].rearrange("b (q e) -> b q e", e=2)
            pv = ps[:].rearrange("b (e q) -> b q e", e=2)
            if u == 0:
                nc.vector.tensor_copy(out=ov, in_=pv)
            else:
                nc.scalar.copy(out=ov, in_=pv)
            nc.sync.dma_start(out=out[:, 2 * P * u:2 * P * (u + 1)], in_=out_sb[:, 2 * P * u:2 * P * (u + 1)])
